import numpy as np
import ml_dtypes


def mxq(x, axis, fmt="e4m3"):
    dtype, down = {"e4m3": (ml_dtypes.float8_e4m3fn, 7), "e5m2": (ml_dtypes.float8_e5m2, 14)}[fmt]
    v = np.moveaxis(np.asarray(x, np.float32).astype(ml_dtypes.bfloat16).astype(np.float64), axis, -1)
    blocks = v.reshape(v.shape[:-1] + (-1, 32))
    amax = np.abs(blocks).max(-1, keepdims=True)
    byte = np.maximum(np.where(amax > 0, np.frexp(amax)[1] - 1 + 127, 0) - down, 1)
    scale = np.exp2(byte - 127.0)
    codes = (blocks / scale).astype(np.float32).astype(dtype).astype(np.float64)
    return np.moveaxis((codes * scale).reshape(v.shape), -1, axis)


WIDE = False


def mx_kscale(k):
    if not WIDE:
        return np.ones(k)
    levels = np.array([10, -10, 5, -5, 0])
    a = np.random.permutation(np.resize(levels, k // 512 * 4)).reshape(k // 512, 4)
    idx = np.arange(k)
    return np.exp2(a[idx // 512, idx % 128 // 32])


BF16 = ml_dtypes.bfloat16


def bf(x):
    return np.asarray(x, np.float32).astype(BF16)


def f64(x):
    return np.asarray(x).astype(np.float64)


E2M1 = np.array([0.0, 0.5, 1.0, 1.5, 2.0, 3.0, 4.0, 6.0, -0.0, -0.5, -1.0, -1.5, -2.0, -3.0, -4.0, -6.0])


def pack_weight(w, fmt):
    k, n = w.shape
    w = f64(bf(w)).reshape(k // 32, 32, n)
    amax = np.abs(w).max(1)
    if fmt == "e4m3":
        byte = np.frexp(amax)[1] - 1 + 127 - 7
    else:
        mant, ex = np.frexp(amax / 6.0)
        byte = np.where(mant > 0.5, ex, ex - 1) + 127
    byte = np.clip(np.where(amax > 0, byte, 1), 1, 254)
    scaled = (w * np.exp2(127.0 - byte)[:, None, :]).reshape(k, n).astype(np.float32)
    by_word = np.ascontiguousarray(scaled.reshape(k // 512, 128, 4, n).transpose(0, 1, 3, 2))
    if fmt == "e4m3":
        words = by_word.astype(ml_dtypes.float8_e4m3fn).view(np.uint8)
    else:
        c = by_word.astype(ml_dtypes.float4_e2m1fn).view(np.uint8) & 0xF
        words = c[..., 0::2] | (c[..., 1::2] << 4)
    return np.ascontiguousarray(words), np.ascontiguousarray(byte.astype(np.uint8).reshape(k // 512, 16, n))


def unpack_weight(words, scales, fmt):
    g, p, n, _ = words.shape
    if fmt == "e4m3":
        vals = np.ascontiguousarray(words).view(ml_dtypes.float8_e4m3fn).astype(np.float64)
    else:
        nib = np.empty((g, p, n, 4), np.uint8)
        nib[..., 0::2] = words & 0xF
        nib[..., 1::2] = words >> 4
        vals = E2M1[nib]
    vals = vals * np.repeat(np.exp2(scales.astype(np.float64) - 127.0), 8, axis=1)[..., None]
    return vals.transpose(0, 1, 3, 2).reshape(g * 512, n)


T, B, D, H, HD, A = 256, 1, 16384, 16, 16, 16
HH = H * HD
HA = H * A
N = HH + HH + HA + HA
EPS = 1e-5
QK = 1.5


def layer_norm(x, w, b):
    mu = x.mean(-1, keepdims=True)
    var = np.square(x - mu).mean(-1, keepdims=True)
    return (x - mu) * (1.0 / np.sqrt(var + EPS)) * w + b


def setup_inputs():
    s = mx_kscale(D)
    col = np.concatenate([np.ones(HH + HH), QK * np.ones(HA + HA)])
    src = bf(np.random.standard_normal((T, B, D)))
    ln1_w = bf((1.0 + 0.1 * np.random.standard_normal(D)) * s)
    ln1_b = bf(0.1 * np.random.standard_normal(D) * s)
    words, scales = pack_weight(np.random.standard_normal((D, N)) * col / np.sqrt(D) / s[:, None], "e4m3")
    b_uvqk = bf(0.1 * np.random.standard_normal(N))
    return {"src": src,
            "ln1_w": ln1_w,
            "ln1_b": ln1_b,
            "w_uvqk_words": words,
            "w_uvqk_scales": scales,
            "b_uvqk": b_uvqk}


def reference(src, ln1_w, ln1_b, w_uvqk_words, w_uvqk_scales, b_uvqk):
    src_norm = layer_norm(f64(src), f64(ln1_w), f64(ln1_b))
    return (mxq(src_norm, 2, "e4m3") @ unpack_weight(w_uvqk_words, w_uvqk_scales, "e4m3")) + f64(b_uvqk)

@@ -1,0 +1,281 @@
+import concourse.mybir as mybir
+from concourse.masks import make_identity
+
+F32 = mybir.dt.float32
+BF16 = mybir.dt.bfloat16
+I32 = mybir.dt.int32
+U32 = mybir.dt.uint32
+U8 = mybir.dt.uint8
+FP8X4 = mybir.dt.float8_e4m3fn_x4
+ALU = mybir.AluOpType
+ACT = mybir.ActivationFunctionType
+
+P = 128
+PACK = 4
+K_PASS = P * PACK
+TOKENS, D, N = 256, 16384, 1024
+EPS = 1e-5
+TOKEN_TILES = TOKENS // P
+GROUPS = D // K_PASS
+N_HALF = 512
+HALVES = N // N_HALF
+BATCH = 4
+BATCH_COLS = BATCH * K_PASS
+BATCHES = GROUPS // BATCH
+SLAB_COLS = 4 * BATCH_COLS
+SLAB_BATCHES = SLAB_COLS // BATCH_COLS
+RESIDENT_SLABS = 10
+VECTOR_PIECES = (512, 512, 384)
+SCALAR_COLS = BATCH_COLS - sum(VECTOR_PIECES)
+SCALAR_COUNT = BATCHES * SCALAR_COLS
+STAT_COLS = 6 * len(VECTOR_PIECES) * BATCHES
+MULTIPLY_LAG = 2
+
+FLOPS = 2 * TOKENS * D * N
+
+
+def tile_stulayer_pa_k_kernel(tc, src, ln1_w, ln1_b, w_uvqk_words, w_uvqk_scales, b_uvqk, out):
+    nc = tc.nc
+    src_rows = src.rearrange("t b d -> (t b) d")
+    out_rows = out.rearrange("t b n -> (t b) n")
+
+    with tc.manual_schedule(), tc.tile_pool(name="const", bufs=1) as const, tc.tile_pool(
+        name="slabs", bufs=RESIDENT_SLABS
+    ) as slabs, tc.tile_pool(name="stats", bufs=1) as stats, tc.tile_pool(name="ring", bufs=2) as ring, tc.tile_pool(
+        name="codes", bufs=MULTIPLY_LAG + 1
+    ) as code_ring, tc.psum_pool(name="turned", bufs=6) as turned, tc.psum_pool(name="sums", bufs=1) as sums:
+
+        ident = const.tile([P, P], F32)
+        make_identity(nc, ident[:])
+
+        gain_rows = const.tile([P, K_PASS], BF16)
+        nc.vector.memset(gain_rows[64:128, :], 0.0)
+        nc.scalar.dma_start(out=gain_rows[0:GROUPS, :], in_=ln1_w.rearrange("(g k) -> g k", k=K_PASS))
+        nc.scalar.dma_start(out=gain_rows[GROUPS : 2 * GROUPS, :], in_=ln1_b.rearrange("(g k) -> g k", k=K_PASS))
+        bias_row = const.tile([P, N], BF16)
+        nc.vector.memset(bias_row[:], 0.0)
+        nc.scalar.dma_start(out=bias_row[0:1, :], in_=b_uvqk.rearrange("(o n) -> o n", o=1))
+        ones = const.tile([P, P], BF16)
+        nc.vector.memset(ones[:], 1.0)
+
+        one = const.tile([P, 1], F32)
+        nc.vector.memset(one[:], 1.0)
+        warm = const.tile([P, 1], F32)
+        nc.scalar.activation(out=warm[:], in_=one[:], func=ACT.Sqrt)
+
+        def load_src(i):
+            pair = []
+            for half in range(D // SLAB_COLS):
+                slab = slabs.tile([P, SLAB_COLS], BF16, tag="slab", name="src_slab", align_bytes=64)
+                for part in range(2):
+                    cols = slice(part * SLAB_COLS // 2, (part + 1) * SLAB_COLS // 2)
+                    first = half * SLAB_COLS + part * SLAB_COLS // 2
+                    nc.sync.dma_start(
+                        out=slab[:, cols], in_=src_rows[i * P : (i + 1) * P, first : first + SLAB_COLS // 2]
+                    )
+                pair.append(slab)
+            return pair
+
+        w_planes = const.tile([P, BATCHES, N], U8, align_bytes=64)
+        nc.vector.memset(w_planes[:].rearrange("p c n -> p (c n)").bitcast(I32), 0)
+
+        def load_weights(c):
+            groups = slice(c * BATCH, (c + 1) * BATCH)
+            for q in range(4):
+                nc.sync.dma_start(
+                    out=w_planes[32 * q : 32 * q + 16, c, :].bitcast(I32),
+                    in_=w_uvqk_scales[groups, 4 * q : 4 * q + 4, :].bitcast(I32),
+                )
+            words = slabs.tile([P, BATCH, N], U32, tag="slab", name="w_slab", align_bytes=64)
+            nc.sync.dma_start(
+                out=words[:].bitcast(I32),
+                in_=w_uvqk_words[groups].rearrange("g p n t -> p g (n t)").bitcast(I32),
+            )
+            return words
+
+        x = [load_src(i) for i in range(TOKEN_TILES)]
+        w_words = [load_weights(c) for c in range(RESIDENT_SLABS - 2 * TOKEN_TILES)]
+
+        gain_sorted = const.tile([P, PACK, P], F32)
+        nc.vector.tensor_copy(out=gain_sorted[:], in_=gain_rows[:].rearrange("r (p t) -> r t p", t=PACK))
+        gain_turned = turned.tile([P, PACK, P], F32, tag="turned")
+        for t in range(PACK):
+            nc.tensor.transpose(gain_turned[:, t, :], gain_sorted[:, t, :], ident[:])
+        bias_spread = []
+        for h in range(HALVES):
+            spread = turned.tile([P, N_HALF], F32, tag="turned")
+            nc.tensor.matmul(
+                spread[:], lhsT=ones[:], rhs=bias_row[:, h * N_HALF : (h + 1) * N_HALF], start=True, stop=True
+            )
+            bias_spread.append(spread)
+        gain_col = const.tile([P, PACK, GROUPS], F32)
+        shift_col = const.tile([P, PACK, GROUPS], F32)
+        bias_all = const.tile([P, N], F32)
+
+        def keep_constants():
+            nc.scalar.copy(out=gain_col[:], in_=gain_turned[:, :, 0:GROUPS])
+            nc.scalar.copy(out=shift_col[:], in_=gain_turned[:, :, GROUPS : 2 * GROUPS])
+            for h in range(HALVES):
+                nc.scalar.copy(out=bias_all[:, h * N_HALF : (h + 1) * N_HALF], in_=bias_spread[h][:])
+
+        def batch_cols(i, c):
+            first = (c % SLAB_BATCHES) * BATCH_COLS
+            return x[i][c // SLAB_BATCHES][:, first : first + BATCH_COLS]
+
+        moments, scalar_sums, neg_first = [], [], []
+        unread_sum = stats.tile([P, SCALAR_COLS], BF16)
+        unread_square = stats.tile([P, SCALAR_COLS], BF16)
+        for i in range(TOKEN_TILES):
+            moments.append(stats.tile([P, STAT_COLS + 3], F32, name="moments%d" % i))
+            scalar_sums.append(stats.tile([P, 2, BATCHES], F32, name="scalar_sums%d" % i))
+            neg_first.append(stats.tile([P, 1], F32, name="neg_first%d" % i))
+            nc.vector.memset(moments[i][:, STAT_COLS : STAT_COLS + 1], float(SCALAR_COUNT))
+
+        def start_stats(i):
+            nc.vector.tensor_scalar_mul(out=neg_first[i][:], in0=batch_cols(i, 0)[:, 0:1], scalar1=-1.0)
+
+        def stats_piece(i, c):
+            cols = batch_cols(i, c)
+            first = 0
+            for j, width in enumerate(VECTOR_PIECES):
+                at = 6 * (len(VECTOR_PIECES) * c + j)
+                nc.vector.bn_stats(out=moments[i][:, at : at + 6], in_=cols[:, first : first + width])
+                first += width
+            nc.scalar.activation(
+                out=unread_sum[:], in_=cols[:, first:BATCH_COLS], func=ACT.Identity, bias=neg_first[i][:],
+                accum_out=scalar_sums[i][:, 0, c : c + 1],
+            )
+            nc.scalar.activation(
+                out=unread_square[:], in_=cols[:, first:BATCH_COLS], func=ACT.Square, bias=neg_first[i][:],
+                accum_out=scalar_sums[i][:, 1, c : c + 1],
+            )
+
+        def finish_stats(i):
+            total = stats.tile([P, 2], F32, name="total%d" % i)
+            nc.vector.tensor_reduce(out=total[:], in_=scalar_sums[i][:], axis=mybir.AxisListType.X, op=ALU.add)
+            nc.vector.tensor_scalar(
+                out=moments[i][:, STAT_COLS + 1 : STAT_COLS + 2], in0=total[:, 0:1],
+                scalar1=1.0 / SCALAR_COUNT, scalar2=neg_first[i][:], op0=ALU.mult, op1=ALU.subtract,
+            )
+            scaled = stats.tile([P, 1], F32, name="scaled%d" % i)
+            nc.vector.tensor_scalar_mul(out=scaled[:], in0=total[:, 0:1], scalar1=-1.0 / SCALAR_COUNT)
+            nc.vector.tensor_scalar(
+                out=moments[i][:, STAT_COLS + 2 : STAT_COLS + 3], in0=total[:, 0:1],
+                scalar1=scaled[:], scalar2=total[:, 1:2], op0=ALU.mult, op1=ALU.add,
+            )
+            mean_var = stats.tile([P, 2], F32, name="mean_var%d" % i)
+            nc.vector.bn_aggr(out=mean_var[:], in_=moments[i][:])
+            var_eps = stats.tile([P, 1], F32, name="var_eps%d" % i)
+            nc.vector.tensor_scalar_add(out=var_eps[:], in0=mean_var[:, 1:2], scalar1=EPS)
+            std = stats.tile([P, 1], F32, name="std%d" % i)
+            nc.scalar.activation(out=std[:], in_=var_eps[:], func=ACT.Sqrt)
+            rstd = stats.tile([P, 1], F32, name="rstd%d" % i)
+            nc.vector.reciprocal(out=rstd[:], in_=std[:])
+            return mean_var[:, 0:1], rstd[:]
+
+        order = [(i, c) for i in range(TOKEN_TILES) for c in range(BATCHES)]
+        token_stats = {}
+        live = {}
+        acc = {}
+
+        def normalise(s):
+            i, c = order[s]
+            mean, rstd = token_stats[i]
+            z = ring.tile([P, BATCH, PACK, P], F32, name="z")
+            nc.vector.tensor_scalar(
+                out=z[:], in0=batch_cols(i, c).rearrange("k (g p t) -> k g t p", p=P, t=PACK),
+                scalar1=mean, scalar2=rstd, op0=ALU.subtract, op1=ALU.mult,
+            )
+            live["z", s] = z
+
+        def transpose(s):
+            banks = []
+            for g in range(BATCH):
+                z_turned = turned.tile([P, PACK, P], F32, tag="turned")
+                for t in range(PACK):
+                    nc.tensor.transpose(z_turned[:, t, :], live["z", s][:, g, t, :], ident[:])
+                banks.append(z_turned)
+            live["turned", s] = banks
+
+        def scale_shift(s):
+            c = order[s][1]
+            y = ring.tile([P, BATCH, PACK, P], BF16, name="y")
+            for g in range(BATCH):
+                for t in range(PACK):
+                    at = c * BATCH + g
+                    nc.scalar.activation(
+                        out=y[:, g, t, :], in_=live["turned", s][g][:, t, :], func=ACT.Identity,
+                        scale=gain_col[:, t, at : at + 1], bias=shift_col[:, t, at : at + 1],
+                    )
+            live["y", s] = y
+
+        def regroup(s):
+            grouped = ring.tile([P, BATCH, P, PACK], BF16, name="grouped", align_bytes=64)
+            nc.vector.tensor_copy(out=grouped[:], in_=live["y", s][:].rearrange("p g t k -> p g k t"))
+            live["grouped", s] = grouped
+
+        def quantise(s):
+            words = code_ring.tile([P, BATCH * P], U32, name="x_words", align_bytes=64)
+            scales = code_ring.tile([P, BATCH * P], U8, name="x_scales", align_bytes=64)
+            nc.vector.quantize_mx(
+                out=words[:].bitcast(FP8X4), scales=scales[:],
+                in_=live["grouped", s][:].rearrange("p g k t -> p (g k t)"),
+            )
+            live["x", s] = (words, scales)
+
+        def multiply(s):
+            i, c = order[s]
+            words, scales = live["x", s]
+            if c == 0:
+                for h in range(HALVES):
+                    acc[h] = sums.tile([P, N_HALF], F32, name="acc%d" % h)
+            for g in range(BATCH):
+                tokens = slice(g * P, (g + 1) * P)
+                for h in range(HALVES):
+                    cols = slice(h * N_HALF, (h + 1) * N_HALF)
+                    nc.tensor.matmul_mx(
+                        out=acc[h][:],
+                        lhsT=words[:, tokens].bitcast(FP8X4),
+                        lhsT_scale=scales[:, tokens],
+                        rhs=w_words[c][:, g, cols].bitcast(FP8X4),
+                        rhs_scale=w_planes[PACK * g : P, c, cols],
+                        start=(c == 0 and g == 0),
+                        stop=(c == BATCHES - 1 and g == BATCH - 1),
+                    )
+
+        def store(i):
+            for h in range(HALVES):
+                cols = slice(h * N_HALF, (h + 1) * N_HALF)
+                result = ring.tile([P, N_HALF], F32, name="result")
+                nc.vector.tensor_tensor(out=result[:], in0=acc[h][:], in1=bias_all[:, cols], op=ALU.add)
+                nc.sync.dma_start(out=out_rows[i * P : (i + 1) * P, cols], in_=result[:])
+
+        start_stats(0)
+        for c in range(BATCHES):
+            stats_piece(0, c)
+        token_stats[0] = finish_stats(0)
+        keep_constants()
+        start_stats(1)
+        normalise(0)
+
+        steps = len(order)
+        for s in range(steps + MULTIPLY_LAG):
+            if s < steps:
+                transpose(s)
+                scale_shift(s)
+            if 1 <= s <= steps:
+                regroup(s - 1)
+            if s < BATCHES:
+                stats_piece(1, s)
+            if 1 <= s <= steps:
+                quantise(s - 1)
+            if s == BATCHES - 1:
+                token_stats[1] = finish_stats(1)
+            if s + 1 < steps:
+                normalise(s + 1)
+                if order[s + 1][0] == 0 and (order[s + 1][1] + 1) % SLAB_BATCHES == 0:
+                    w_words.append(load_weights(len(w_words)))
+            if s >= MULTIPLY_LAG:
+                multiply(s - MULTIPLY_LAG)
+                if order[s - MULTIPLY_LAG][1] == BATCHES - 1:
+                    store(order[s - MULTIPLY_LAG][0])

@@ -1,3 +1,5 @@
+from contextlib import ExitStack
+
 import concourse.mybir as mybir
 from concourse.masks import make_identity
 
@@ -22,10 +24,10 @@ HALVES = N // N_HALF
 BATCH = 4
 BATCH_COLS = BATCH * K_PASS
 BATCHES = GROUPS // BATCH
-SLAB_COLS = 4 * BATCH_COLS
-SLAB_BATCHES = SLAB_COLS // BATCH_COLS
-RESIDENT_SLABS = 10
-VECTOR_PIECES = (512, 512, 384)
+SLAB_BATCHES = 4
+SLAB_COLS = SLAB_BATCHES * BATCH_COLS
+RESIDENT_SLABS = 11
+VECTOR_PIECES = (512, 512, 512)
 SCALAR_COLS = BATCH_COLS - sum(VECTOR_PIECES)
 SCALAR_COUNT = BATCHES * SCALAR_COLS
 STAT_COLS = 6 * len(VECTOR_PIECES) * BATCHES
@@ -39,78 +41,84 @@ def tile_stulayer_pa_k_kernel(tc, src, ln1_w, ln1_b, w_uvqk_words, w_uvqk_scales
     src_rows = src.rearrange("t b d -> (t b) d")
     out_rows = out.rearrange("t b n -> (t b) n")
 
-    with tc.manual_schedule(), tc.tile_pool(name="const", bufs=1) as const, tc.tile_pool(
-        name="slabs", bufs=RESIDENT_SLABS
-    ) as slabs, tc.tile_pool(name="stats", bufs=1) as stats, tc.tile_pool(name="ring", bufs=2) as ring, tc.tile_pool(
-        name="codes", bufs=MULTIPLY_LAG + 1
-    ) as code_ring, tc.psum_pool(name="turned", bufs=6) as turned, tc.psum_pool(name="sums", bufs=1) as sums:
-
-        ident = const.tile([P, P], F32)
-        make_identity(nc, ident[:])
-
-        gain_rows = const.tile([P, K_PASS], BF16)
-        nc.vector.memset(gain_rows[64:128, :], 0.0)
-        nc.scalar.dma_start(out=gain_rows[0:GROUPS, :], in_=ln1_w.rearrange("(g k) -> g k", k=K_PASS))
-        nc.scalar.dma_start(out=gain_rows[GROUPS : 2 * GROUPS, :], in_=ln1_b.rearrange("(g k) -> g k", k=K_PASS))
-        bias_row = const.tile([P, N], BF16)
-        nc.vector.memset(bias_row[:], 0.0)
-        nc.scalar.dma_start(out=bias_row[0:1, :], in_=b_uvqk.rearrange("(o n) -> o n", o=1))
-        ones = const.tile([P, P], BF16)
-        nc.vector.memset(ones[:], 1.0)
-
-        one = const.tile([P, 1], F32)
-        nc.vector.memset(one[:], 1.0)
-        warm = const.tile([P, 1], F32)
-        nc.scalar.activation(out=warm[:], in_=one[:], func=ACT.Sqrt)
+    with ExitStack() as pools:
+        pools.enter_context(tc.manual_schedule())
+        const = pools.enter_context(tc.tile_pool(name="const", bufs=1))
+        slabs = pools.enter_context(tc.tile_pool(name="slabs", bufs=RESIDENT_SLABS))
+        stats = pools.enter_context(tc.tile_pool(name="stats", bufs=1))
+        turned = pools.enter_context(tc.psum_pool(name="turned", bufs=6))
+        sums = pools.enter_context(tc.psum_pool(name="sums", bufs=1))
 
         def load_src(i):
             pair = []
             for half in range(D // SLAB_COLS):
                 slab = slabs.tile([P, SLAB_COLS], BF16, tag="slab", name="src_slab", align_bytes=64)
-                for part in range(2):
-                    cols = slice(part * SLAB_COLS // 2, (part + 1) * SLAB_COLS // 2)
-                    first = half * SLAB_COLS + part * SLAB_COLS // 2
-                    nc.sync.dma_start(
-                        out=slab[:, cols], in_=src_rows[i * P : (i + 1) * P, first : first + SLAB_COLS // 2]
-                    )
+                for b in range(SLAB_BATCHES):
+                    cols = slice(b * BATCH_COLS, (b + 1) * BATCH_COLS)
+                    first = half * SLAB_COLS + b * BATCH_COLS
+                    nc.sync.dma_start(out=slab[:, cols], in_=src_rows[i * P : (i + 1) * P, first : first + BATCH_COLS])
                 pair.append(slab)
             return pair
 
-        w_planes = const.tile([P, BATCHES, N], U8, align_bytes=64)
-        nc.vector.memset(w_planes[:].rearrange("p c n -> p (c n)").bitcast(I32), 0)
-
-        def load_weights(c):
-            groups = slice(c * BATCH, (c + 1) * BATCH)
-            for q in range(4):
-                nc.sync.dma_start(
-                    out=w_planes[32 * q : 32 * q + 16, c, :].bitcast(I32),
-                    in_=w_uvqk_scales[groups, 4 * q : 4 * q + 4, :].bitcast(I32),
-                )
+        def load_words(c):
             words = slabs.tile([P, BATCH, N], U32, tag="slab", name="w_slab", align_bytes=64)
             nc.sync.dma_start(
                 out=words[:].bitcast(I32),
-                in_=w_uvqk_words[groups].rearrange("g p n t -> p g (n t)").bitcast(I32),
+                in_=w_uvqk_words[c * BATCH : (c + 1) * BATCH].rearrange("g p n t -> p g (n t)").bitcast(I32),
             )
             return words
 
-        x = [load_src(i) for i in range(TOKEN_TILES)]
-        w_words = [load_weights(c) for c in range(RESIDENT_SLABS - 2 * TOKEN_TILES)]
-
-        gain_sorted = const.tile([P, PACK, P], F32)
-        nc.vector.tensor_copy(out=gain_sorted[:], in_=gain_rows[:].rearrange("r (p t) -> r t p", t=PACK))
-        gain_turned = turned.tile([P, PACK, P], F32, tag="turned")
-        for t in range(PACK):
-            nc.tensor.transpose(gain_turned[:, t, :], gain_sorted[:, t, :], ident[:])
-        bias_spread = []
-        for h in range(HALVES):
-            spread = turned.tile([P, N_HALF], F32, tag="turned")
-            nc.tensor.matmul(
-                spread[:], lhsT=ones[:], rhs=bias_row[:, h * N_HALF : (h + 1) * N_HALF], start=True, stop=True
-            )
-            bias_spread.append(spread)
+        ident = const.tile([P, P], F32)
         gain_col = const.tile([P, PACK, GROUPS], F32)
         shift_col = const.tile([P, PACK, GROUPS], F32)
-        bias_all = const.tile([P, N], F32)
+        bias_all = const.tile([P, N], BF16)
+        w_planes = const.tile([P, BATCHES, N], U8, align_bytes=64)
+        bias_spread = []
+
+        with tc.tile_pool(name="setup", bufs=1) as setup:
+            make_identity(nc, ident[:])
+
+            gain_rows = setup.tile([P, K_PASS], BF16)
+            nc.vector.memset(gain_rows[64:128, :], 0.0)
+            nc.scalar.dma_start(out=gain_rows[0:GROUPS, :], in_=ln1_w.rearrange("(g k) -> g k", k=K_PASS))
+            nc.scalar.dma_start(out=gain_rows[GROUPS : 2 * GROUPS, :], in_=ln1_b.rearrange("(g k) -> g k", k=K_PASS))
+            bias_row = setup.tile([P, N], BF16)
+            nc.vector.memset(bias_row[:], 0.0)
+            nc.scalar.dma_start(out=bias_row[0:1, :], in_=b_uvqk.rearrange("(o n) -> o n", o=1))
+            ones = setup.tile([P, P], BF16)
+            nc.vector.memset(ones[:], 1.0)
+
+            one = setup.tile([P, 1], F32)
+            nc.vector.memset(one[:], 1.0)
+            warm = setup.tile([P, 1], F32)
+            nc.scalar.activation(out=warm[:], in_=one[:], func=ACT.Sqrt)
+
+            nc.vector.memset(w_planes[:].rearrange("p c n -> p (c n)").bitcast(I32), 0)
+            scale_rows = w_uvqk_scales.rearrange("(c j) q n -> j q c n", j=BATCH)
+            for j in range(BATCH):
+                for q in range(4):
+                    at = 32 * q + PACK * j
+                    nc.gpsimd.dma_start(
+                        out=w_planes[at : at + 4, :, :].bitcast(F32), in_=scale_rows[j, 4 * q : 4 * q + 4].bitcast(F32)
+                    )
+
+            x = [load_src(i) for i in range(TOKEN_TILES)]
+            w_words = [load_words(c) for c in range(BATCHES - 1)]
+
+            gain_sorted = setup.tile([P, PACK, P], F32)
+            nc.vector.tensor_copy(out=gain_sorted[:], in_=gain_rows[:].rearrange("r (p t) -> r t p", t=PACK))
+            gain_turned = turned.tile([P, PACK, P], F32, tag="turned")
+            for t in range(PACK):
+                nc.tensor.transpose(gain_turned[:, t, :], gain_sorted[:, t, :], ident[:])
+            for h in range(HALVES):
+                spread = turned.tile([P, N_HALF], F32, tag="turned")
+                nc.tensor.matmul(
+                    spread[:], lhsT=ones[:], rhs=bias_row[:, h * N_HALF : (h + 1) * N_HALF], start=True, stop=True
+                )
+                bias_spread.append(spread)
+
+        ring = pools.enter_context(tc.tile_pool(name="ring", bufs=2))
+        code_ring = pools.enter_context(tc.tile_pool(name="codes", bufs=MULTIPLY_LAG + 1))
 
         def keep_constants():
             nc.scalar.copy(out=gain_col[:], in_=gain_turned[:, :, 0:GROUPS])
@@ -211,7 +219,10 @@ def tile_stulayer_pa_k_kernel(tc, src, ln1_w, ln1_b, w_uvqk_words, w_uvqk_scales
 
         def regroup(s):
             grouped = ring.tile([P, BATCH, P, PACK], BF16, name="grouped", align_bytes=64)
-            nc.vector.tensor_copy(out=grouped[:], in_=live["y", s][:].rearrange("p g t k -> p g k t"))
+            nc.vector.tensor_copy(
+                out=grouped[:].rearrange("p g (c i) t -> p g c t i", i=4),
+                in_=live["y", s][:].rearrange("p g t (c i) -> p g c t i", i=4),
+            )
             live["grouped", s] = grouped
 
         def quantise(s):
@@ -229,10 +240,10 @@ def tile_stulayer_pa_k_kernel(tc, src, ln1_w, ln1_b, w_uvqk_words, w_uvqk_scales
             if c == 0:
                 for h in range(HALVES):
                     acc[h] = sums.tile([P, N_HALF], F32, name="acc%d" % h)
-            for g in range(BATCH):
-                tokens = slice(g * P, (g + 1) * P)
-                for h in range(HALVES):
-                    cols = slice(h * N_HALF, (h + 1) * N_HALF)
+            for h in range(HALVES):
+                cols = slice(h * N_HALF, (h + 1) * N_HALF)
+                for g in range(BATCH):
+                    tokens = slice(g * P, (g + 1) * P)
                     nc.tensor.matmul_mx(
                         out=acc[h][:],
                         lhsT=words[:, tokens].bitcast(FP8X4),
@@ -255,8 +266,9 @@ def tile_stulayer_pa_k_kernel(tc, src, ln1_w, ln1_b, w_uvqk_words, w_uvqk_scales
             stats_piece(0, c)
         token_stats[0] = finish_stats(0)
         keep_constants()
-        start_stats(1)
         normalise(0)
+        start_stats(1)
+        stats_piece(1, 0)
 
         steps = len(order)
         for s in range(steps + MULTIPLY_LAG):
@@ -265,16 +277,16 @@ def tile_stulayer_pa_k_kernel(tc, src, ln1_w, ln1_b, w_uvqk_words, w_uvqk_scales
                 scale_shift(s)
             if 1 <= s <= steps:
                 regroup(s - 1)
-            if s < BATCHES:
-                stats_piece(1, s)
+            if s + 1 < BATCHES:
+                stats_piece(1, s + 1)
             if 1 <= s <= steps:
                 quantise(s - 1)
             if s == BATCHES - 1:
                 token_stats[1] = finish_stats(1)
             if s + 1 < steps:
                 normalise(s + 1)
-                if order[s + 1][0] == 0 and (order[s + 1][1] + 1) % SLAB_BATCHES == 0:
-                    w_words.append(load_weights(len(w_words)))
+                if s + 1 == SLAB_BATCHES - 1:
+                    w_words.append(load_words(BATCHES - 1))
             if s >= MULTIPLY_LAG:
                 multiply(s - MULTIPLY_LAG)
                 if order[s - MULTIPLY_LAG][1] == BATCHES - 1:

@@ -94,15 +94,14 @@ def tile_stulayer_pa_k_kernel(tc, src, ln1_w, ln1_b, w_uvqk_words, w_uvqk_scales
             nc.scalar.activation(out=warm[:], in_=one[:], func=ACT.Sqrt)
 
             nc.vector.memset(w_planes[:].rearrange("p c n -> p (c n)").bitcast(I32), 0)
-            scale_rows = w_uvqk_scales.rearrange("(c j) q n -> j q c n", j=BATCH)
-            for j in range(BATCH):
+            x = [load_src(0)]
+            for c in range(BATCHES):
                 for q in range(4):
-                    at = 32 * q + PACK * j
-                    nc.gpsimd.dma_start(
-                        out=w_planes[at : at + 4, :, :].bitcast(F32), in_=scale_rows[j, 4 * q : 4 * q + 4].bitcast(F32)
+                    nc.sync.dma_start(
+                        out=w_planes[32 * q : 32 * q + 16, c, :].bitcast(I32),
+                        in_=w_uvqk_scales[c * BATCH : (c + 1) * BATCH, 4 * q : 4 * q + 4, :].bitcast(I32),
                     )
-
-            x = [load_src(i) for i in range(TOKEN_TILES)]
+            x.append(load_src(1))
             w_words = [load_words(c) for c in range(BATCHES - 1)]
 
             gain_sorted = setup.tile([P, PACK, P], F32)

@@ -62,10 +62,11 @@ def tile_stulayer_pa_k_kernel(tc, src, ln1_w, ln1_b, w_uvqk_words, w_uvqk_scales
 
         def load_words(c):
             words = slabs.tile([P, BATCH, N], U32, tag="slab", name="w_slab", align_bytes=64)
-            nc.sync.dma_start(
-                out=words[:].bitcast(I32),
-                in_=w_uvqk_words[c * BATCH : (c + 1) * BATCH].rearrange("g p n t -> p g (n t)").bitcast(I32),
-            )
+            for g in range(BATCH):
+                nc.sync.dma_start(
+                    out=words[:, g, :].bitcast(I32),
+                    in_=w_uvqk_words[c * BATCH + g].rearrange("p n t -> p (n t)").bitcast(I32),
+                )
             return words
 
         ident = const.tile([P, P], F32)
@@ -129,6 +130,8 @@ def tile_stulayer_pa_k_kernel(tc, src, ln1_w, ln1_b, w_uvqk_words, w_uvqk_scales
             first = (c % SLAB_BATCHES) * BATCH_COLS
             return x[i][c // SLAB_BATCHES][:, first : first + BATCH_COLS]
 
+        eps = stats.tile([P, 1], F32)
+        nc.vector.memset(eps[:], EPS)
         moments, scalar_sums, neg_first = [], [], []
         unread_sum = stats.tile([P, SCALAR_COLS], BF16)
         unread_square = stats.tile([P, SCALAR_COLS], BF16)
@@ -172,10 +175,8 @@ def tile_stulayer_pa_k_kernel(tc, src, ln1_w, ln1_b, w_uvqk_words, w_uvqk_scales
             )
             mean_var = stats.tile([P, 2], F32, name="mean_var%d" % i)
             nc.vector.bn_aggr(out=mean_var[:], in_=moments[i][:])
-            var_eps = stats.tile([P, 1], F32, name="var_eps%d" % i)
-            nc.vector.tensor_scalar_add(out=var_eps[:], in0=mean_var[:, 1:2], scalar1=EPS)
             std = stats.tile([P, 1], F32, name="std%d" % i)
-            nc.scalar.activation(out=std[:], in_=var_eps[:], func=ACT.Sqrt)
+            nc.scalar.activation(out=std[:], in_=mean_var[:, 1:2], func=ACT.Sqrt, bias=eps[:])
             rstd = stats.tile([P, 1], F32, name="rstd%d" % i)
             nc.vector.reciprocal(out=rstd[:], in_=std[:])
             return mean_var[:, 0:1], rstd[:]
@@ -239,10 +240,10 @@ def tile_stulayer_pa_k_kernel(tc, src, ln1_w, ln1_b, w_uvqk_words, w_uvqk_scales
             if c == 0:
                 for h in range(HALVES):
                     acc[h] = sums.tile([P, N_HALF], F32, name="acc%d" % h)
-            for h in range(HALVES):
-                cols = slice(h * N_HALF, (h + 1) * N_HALF)
-                for g in range(BATCH):
-                    tokens = slice(g * P, (g + 1) * P)
+            for g in range(BATCH):
+                tokens = slice(g * P, (g + 1) * P)
+                for h in range(HALVES):
+                    cols = slice(h * N_HALF, (h + 1) * N_HALF)
                     nc.tensor.matmul_mx(
                         out=acc[h][:],
                         lhsT=words[:, tokens].bitcast(FP8X4),
@@ -276,16 +277,16 @@ def tile_stulayer_pa_k_kernel(tc, src, ln1_w, ln1_b, w_uvqk_words, w_uvqk_scales
                 scale_shift(s)
             if 1 <= s <= steps:
                 regroup(s - 1)
-            if s + 1 < BATCHES:
-                stats_piece(1, s + 1)
-            if 1 <= s <= steps:
-                quantise(s - 1)
             if s == BATCHES - 1:
                 token_stats[1] = finish_stats(1)
             if s + 1 < steps:
                 normalise(s + 1)
                 if s + 1 == SLAB_BATCHES - 1:
                     w_words.append(load_words(BATCHES - 1))
+            if s + 1 < BATCHES:
+                stats_piece(1, s + 1)
+            if 1 <= s <= steps:
+                quantise(s - 1)
             if s >= MULTIPLY_LAG:
                 multiply(s - MULTIPLY_LAG)
                 if order[s - MULTIPLY_LAG][1] == BATCHES - 1:

@@ -27,13 +27,29 @@ BATCHES = GROUPS // BATCH
 SLAB_BATCHES = 4
 SLAB_COLS = SLAB_BATCHES * BATCH_COLS
 RESIDENT_SLABS = 11
-VECTOR_PIECES = (512, 512, 512)
-SCALAR_COLS = BATCH_COLS - sum(VECTOR_PIECES)
-SCALAR_COUNT = BATCHES * SCALAR_COLS
-STAT_COLS = 6 * len(VECTOR_PIECES) * BATCHES
+PIECE = 512
+PIECE_BLOCKS = PIECE // P
+VECTOR_PIECES = ((2, 2, 2, 2, 2, 2, 3, 3), (2, 2, 2, 2, 2, 2, 2, 2))
+PIECES = BATCH_COLS // PIECE
+AHEAD = 5
+TENSOR_COUNT = [PIECE * sum(PIECES - v for v in row) for row in VECTOR_PIECES]
+STAT_COLS = [6 * sum(row) for row in VECTOR_PIECES]
+GRAM_COLS = P + 2
+RAW_BUFFERS = 4
+GRAM_LAG = 2
 MULTIPLY_LAG = 2
 
 FLOPS = 2 * TOKENS * D * N
+
+
+def work_order():
+    items = [(0, 0, 1), (0, 1, 1), (0, 2, 2)]
+    items += [(0, BATCH * c, BATCH) for c in range(1, AHEAD)]
+    for c in range(BATCHES - AHEAD):
+        items += [(1, BATCH * c, BATCH), (0, BATCH * (AHEAD + c), BATCH)]
+    items += [(1, BATCH * c, BATCH) for c in range(BATCHES - AHEAD, BATCHES - 1)]
+    items += [(1, GROUPS - 4, 2), (1, GROUPS - 2, 1), (1, GROUPS - 1, 1)]
+    return items
 
 
 def tile_stulayer_pa_k_kernel(tc, src, ln1_w, ln1_b, w_uvqk_words, w_uvqk_scales, b_uvqk, out):
@@ -46,7 +62,7 @@ def tile_stulayer_pa_k_kernel(tc, src, ln1_w, ln1_b, w_uvqk_words, w_uvqk_scales
         const = pools.enter_context(tc.tile_pool(name="const", bufs=1))
         slabs = pools.enter_context(tc.tile_pool(name="slabs", bufs=RESIDENT_SLABS))
         stats = pools.enter_context(tc.tile_pool(name="stats", bufs=1))
-        turned = pools.enter_context(tc.psum_pool(name="turned", bufs=6))
+        turned = pools.enter_context(tc.psum_pool(name="turned", bufs=4))
         sums = pools.enter_context(tc.psum_pool(name="sums", bufs=1))
 
         def load_src(i):
@@ -60,6 +76,12 @@ def tile_stulayer_pa_k_kernel(tc, src, ln1_w, ln1_b, w_uvqk_words, w_uvqk_scales
                 pair.append(slab)
             return pair
 
+        def load_scales(c, q):
+            nc.sync.dma_start(
+                out=w_planes[32 * q : 32 * q + 16, c, :].bitcast(I32),
+                in_=w_uvqk_scales[c * BATCH : (c + 1) * BATCH, 4 * q : 4 * q + 4, :].bitcast(I32),
+            )
+
         def load_words(c):
             words = slabs.tile([P, BATCH, N], U32, tag="slab", name="w_slab", align_bytes=64)
             for g in range(BATCH):
@@ -67,64 +89,62 @@ def tile_stulayer_pa_k_kernel(tc, src, ln1_w, ln1_b, w_uvqk_words, w_uvqk_scales
                     out=words[:, g, :].bitcast(I32),
                     in_=w_uvqk_words[c * BATCH + g].rearrange("p n t -> p (n t)").bitcast(I32),
                 )
+                if c + 1 < BATCHES:
+                    load_scales(c + 1, g)
             return words
 
         ident = const.tile([P, P], F32)
+        ident_raw = const.tile([P, P], BF16)
         gain_col = const.tile([P, PACK, GROUPS], F32)
         shift_col = const.tile([P, PACK, GROUPS], F32)
         bias_all = const.tile([P, N], BF16)
         w_planes = const.tile([P, BATCHES, N], U8, align_bytes=64)
-        bias_spread = []
+        raw_turned = [const.tile([P, PIECE_BLOCKS, GRAM_COLS], BF16, name="raw_turned%d" % n) for n in range(RAW_BUFFERS)]
 
-        with tc.tile_pool(name="setup", bufs=1) as setup:
-            make_identity(nc, ident[:])
-
-            gain_rows = setup.tile([P, K_PASS], BF16)
-            nc.vector.memset(gain_rows[64:128, :], 0.0)
-            nc.scalar.dma_start(out=gain_rows[0:GROUPS, :], in_=ln1_w.rearrange("(g k) -> g k", k=K_PASS))
-            nc.scalar.dma_start(out=gain_rows[GROUPS : 2 * GROUPS, :], in_=ln1_b.rearrange("(g k) -> g k", k=K_PASS))
-            bias_row = setup.tile([P, N], BF16)
-            nc.vector.memset(bias_row[:], 0.0)
-            nc.scalar.dma_start(out=bias_row[0:1, :], in_=b_uvqk.rearrange("(o n) -> o n", o=1))
-            ones = setup.tile([P, P], BF16)
-            nc.vector.memset(ones[:], 1.0)
-
-            one = setup.tile([P, 1], F32)
-            nc.vector.memset(one[:], 1.0)
-            warm = setup.tile([P, 1], F32)
-            nc.scalar.activation(out=warm[:], in_=one[:], func=ACT.Sqrt)
-
-            nc.vector.memset(w_planes[:].rearrange("p c n -> p (c n)").bitcast(I32), 0)
-            x = [load_src(0)]
-            for c in range(BATCHES):
-                for q in range(4):
-                    nc.sync.dma_start(
-                        out=w_planes[32 * q : 32 * q + 16, c, :].bitcast(I32),
-                        in_=w_uvqk_scales[c * BATCH : (c + 1) * BATCH, 4 * q : 4 * q + 4, :].bitcast(I32),
-                    )
-            x.append(load_src(1))
-            w_words = [load_words(c) for c in range(BATCHES - 1)]
-
-            gain_sorted = setup.tile([P, PACK, P], F32)
-            nc.vector.tensor_copy(out=gain_sorted[:], in_=gain_rows[:].rearrange("r (p t) -> r t p", t=PACK))
-            gain_turned = turned.tile([P, PACK, P], F32, tag="turned")
-            for t in range(PACK):
-                nc.tensor.transpose(gain_turned[:, t, :], gain_sorted[:, t, :], ident[:])
-            for h in range(HALVES):
-                spread = turned.tile([P, N_HALF], F32, tag="turned")
-                nc.tensor.matmul(
-                    spread[:], lhsT=ones[:], rhs=bias_row[:, h * N_HALF : (h + 1) * N_HALF], start=True, stop=True
-                )
-                bias_spread.append(spread)
-
+        setup = pools.enter_context(tc.tile_pool(name="setup", bufs=1))
         ring = pools.enter_context(tc.tile_pool(name="ring", bufs=2))
+        make_identity(nc, ident_raw[:])
+        for tile in raw_turned:
+            nc.gpsimd.memset(tile[:, :, P:GRAM_COLS], 1.0)
+        make_identity(nc, ident[:])
+
+        gain_rows = setup.tile([P, K_PASS], BF16)
+        nc.gpsimd.memset(gain_rows[64:128, :], 0.0)
+        nc.scalar.dma_start(out=gain_rows[0:GROUPS, :], in_=ln1_w.rearrange("(g k) -> g k", k=K_PASS))
+        nc.scalar.dma_start(out=gain_rows[GROUPS : 2 * GROUPS, :], in_=ln1_b.rearrange("(g k) -> g k", k=K_PASS))
+        bias_row = ring.tile([P, N], BF16, tag="result")
+        nc.vector.memset(bias_row[:], 0.0)
+        nc.scalar.dma_start(out=bias_row[0:1, :], in_=b_uvqk.rearrange("(o n) -> o n", o=1))
+        ones = setup.tile([P, P], BF16)
+        nc.vector.memset(ones[:], 1.0)
+
+        one = setup.tile([P, 1], F32)
+        nc.vector.memset(one[:], 1.0)
+        warm = setup.tile([P, 1], F32)
+        nc.scalar.activation(out=warm[:], in_=one[:], func=ACT.Sqrt)
+
+        nc.gpsimd.memset(w_planes[:].rearrange("p c n -> p (c n)").bitcast(I32), 0)
+        x = [load_src(0), load_src(1)]
+        for q in range(4):
+            load_scales(0, q)
+        w_words = [load_words(c) for c in range(BATCHES - 1)]
+
         code_ring = pools.enter_context(tc.tile_pool(name="codes", bufs=MULTIPLY_LAG + 1))
 
-        def keep_constants():
+        def make_constants():
+            gain_sorted = ring.tile([P, PACK, P], F32, tag="result")
+            nc.vector.tensor_copy(out=gain_sorted[:], in_=gain_rows[:].rearrange("r (p t) -> r t p", t=PACK))
+            gain_turned = sums.tile([P, PACK, P], F32, tag="acc0_1")
+            for t in range(PACK):
+                nc.tensor.transpose(gain_turned[:, t, :], gain_sorted[:, t, :], ident[:])
             nc.scalar.copy(out=gain_col[:], in_=gain_turned[:, :, 0:GROUPS])
             nc.scalar.copy(out=shift_col[:], in_=gain_turned[:, :, GROUPS : 2 * GROUPS])
             for h in range(HALVES):
-                nc.scalar.copy(out=bias_all[:, h * N_HALF : (h + 1) * N_HALF], in_=bias_spread[h][:])
+                spread = sums.tile([P, N_HALF], F32, tag="acc1_1")
+                nc.tensor.matmul(
+                    spread[:], lhsT=ones[:], rhs=bias_row[:, h * N_HALF : (h + 1) * N_HALF], start=True, stop=True
+                )
+                nc.scalar.copy(out=bias_all[:, h * N_HALF : (h + 1) * N_HALF], in_=spread[:])
 
         def batch_cols(i, c):
             first = (c % SLAB_BATCHES) * BATCH_COLS
@@ -132,46 +152,72 @@ def tile_stulayer_pa_k_kernel(tc, src, ln1_w, ln1_b, w_uvqk_words, w_uvqk_scales
 
         eps = stats.tile([P, 1], F32)
         nc.vector.memset(eps[:], EPS)
-        moments, scalar_sums, neg_first = [], [], []
-        unread_sum = stats.tile([P, SCALAR_COLS], BF16)
-        unread_square = stats.tile([P, SCALAR_COLS], BF16)
+        moments, gram = [], []
         for i in range(TOKEN_TILES):
-            moments.append(stats.tile([P, STAT_COLS + 3], F32, name="moments%d" % i))
-            scalar_sums.append(stats.tile([P, 2, BATCHES], F32, name="scalar_sums%d" % i))
-            neg_first.append(stats.tile([P, 1], F32, name="neg_first%d" % i))
-            nc.vector.memset(moments[i][:, STAT_COLS : STAT_COLS + 1], float(SCALAR_COUNT))
+            moments.append(stats.tile([P, STAT_COLS[i] + 3], F32, name="moments%d" % i))
+            nc.vector.memset(moments[i][:, STAT_COLS[i] : STAT_COLS[i] + 1], float(TENSOR_COUNT[i]))
+        diagonal = stats.tile([P, P], F32)
 
-        def start_stats(i):
-            nc.vector.tensor_scalar_mul(out=neg_first[i][:], in0=batch_cols(i, 0)[:, 0:1], scalar1=-1.0)
+        def vector_piece(i, c):
+            for j in range(VECTOR_PIECES[i][c]):
+                at = 6 * (sum(VECTOR_PIECES[i][:c]) + j)
+                nc.vector.bn_stats(
+                    out=moments[i][:, at : at + 6], in_=batch_cols(i, c)[:, j * PIECE : (j + 1) * PIECE]
+                )
 
-        def stats_piece(i, c):
-            cols = batch_cols(i, c)
-            first = 0
-            for j, width in enumerate(VECTOR_PIECES):
-                at = 6 * (len(VECTOR_PIECES) * c + j)
-                nc.vector.bn_stats(out=moments[i][:, at : at + 6], in_=cols[:, first : first + width])
-                first += width
-            nc.scalar.activation(
-                out=unread_sum[:], in_=cols[:, first:BATCH_COLS], func=ACT.Identity, bias=neg_first[i][:],
-                accum_out=scalar_sums[i][:, 0, c : c + 1],
-            )
-            nc.scalar.activation(
-                out=unread_square[:], in_=cols[:, first:BATCH_COLS], func=ACT.Square, bias=neg_first[i][:],
-                accum_out=scalar_sums[i][:, 1, c : c + 1],
-            )
+        tensor_pieces = [[(i, c, j) for c in range(BATCHES) for j in range(VECTOR_PIECES[i][c], PIECES)] for i in range(TOKEN_TILES)]
+        turned_pieces = [0]
+
+        raw_ring = []
+
+        def turn_piece(piece):
+            i, c, j = piece
+            bank = turned.tile([P, PIECE_BLOCKS, P], BF16, tag="turned")
+            for b in range(PIECE_BLOCKS):
+                first = j * PIECE + b * P
+                nc.tensor.transpose(bank[:, b, :], batch_cols(i, c)[:, first : first + P], ident_raw[:])
+            tile = raw_turned[len(raw_ring) % len(raw_turned)]
+            nc.scalar.copy(out=tile[:, :, 0:P], in_=bank[:])
+            raw_ring.append((piece, tile))
+
+        summed = []
+
+        def sum_piece():
+            piece, tile = raw_ring[len(summed)]
+            i = piece[0]
+            if piece == tensor_pieces[i][0]:
+                gram.append(sums.tile([P, GRAM_COLS], F32, tag="acc%d_0" % i, name="gram"))
+            for b in range(PIECE_BLOCKS):
+                nc.tensor.matmul(
+                    gram[i][:], lhsT=tile[:, b, 0:P], rhs=tile[:, b, :],
+                    start=(piece == tensor_pieces[i][0] and b == 0),
+                    stop=(piece == tensor_pieces[i][-1] and b == PIECE_BLOCKS - 1),
+                )
+            summed.append(piece)
+
+        def turn_pieces(i, c):
+            for piece in tensor_pieces[i]:
+                if piece[1] == c:
+                    turn_piece(piece)
+
+        def sum_pieces(lag):
+            while len(raw_ring) - len(summed) > lag:
+                sum_piece()
 
         def finish_stats(i):
-            total = stats.tile([P, 2], F32, name="total%d" % i)
-            nc.vector.tensor_reduce(out=total[:], in_=scalar_sums[i][:], axis=mybir.AxisListType.X, op=ALU.add)
-            nc.vector.tensor_scalar(
-                out=moments[i][:, STAT_COLS + 1 : STAT_COLS + 2], in0=total[:, 0:1],
-                scalar1=1.0 / SCALAR_COUNT, scalar2=neg_first[i][:], op0=ALU.mult, op1=ALU.subtract,
+            mean_of_share = moments[i][:, STAT_COLS[i] + 1 : STAT_COLS[i] + 2]
+            total = gram[i][:, P : P + 1]
+            negative = stats.tile([P, 1], F32, name="negative%d" % i)
+            squares = stats.tile([P, 1], F32, name="squares%d" % i)
+            nc.vector.tensor_scalar_mul(out=mean_of_share, in0=total, scalar1=1.0 / TENSOR_COUNT[i])
+            nc.vector.tensor_scalar_mul(out=negative[:], in0=total, scalar1=-1.0 / TENSOR_COUNT[i])
+            nc.vector.scalar_tensor_tensor(
+                out=diagonal[:], in0=gram[i][:, 0:P], scalar=1.0, in1=ident[:], op0=ALU.mult, op1=ALU.mult,
+                accum_out=squares[:],
             )
-            scaled = stats.tile([P, 1], F32, name="scaled%d" % i)
-            nc.vector.tensor_scalar_mul(out=scaled[:], in0=total[:, 0:1], scalar1=-1.0 / SCALAR_COUNT)
             nc.vector.tensor_scalar(
-                out=moments[i][:, STAT_COLS + 2 : STAT_COLS + 3], in0=total[:, 0:1],
-                scalar1=scaled[:], scalar2=total[:, 1:2], op0=ALU.mult, op1=ALU.add,
+                out=moments[i][:, STAT_COLS[i] + 2 : STAT_COLS[i] + 3], in0=total,
+                scalar1=negative[:], scalar2=squares[:], op0=ALU.mult, op1=ALU.add,
             )
             mean_var = stats.tile([P, 2], F32, name="mean_var%d" % i)
             nc.vector.bn_aggr(out=mean_var[:], in_=moments[i][:])
@@ -181,24 +227,29 @@ def tile_stulayer_pa_k_kernel(tc, src, ln1_w, ln1_b, w_uvqk_words, w_uvqk_scales
             nc.vector.reciprocal(out=rstd[:], in_=std[:])
             return mean_var[:, 0:1], rstd[:]
 
-        order = [(i, c) for i in range(TOKEN_TILES) for c in range(BATCHES)]
+        order = work_order()
+        steps = len(order)
+        first_of = {i: min(s for s in range(steps) if order[s][0] == i) for i in range(TOKEN_TILES)}
+        last_of = {i: max(s for s in range(steps) if order[s][0] == i) for i in range(TOKEN_TILES)}
         token_stats = {}
         live = {}
         acc = {}
 
         def normalise(s):
-            i, c = order[s]
+            i, first, count = order[s]
             mean, rstd = token_stats[i]
-            z = ring.tile([P, BATCH, PACK, P], F32, name="z")
+            c, g0 = divmod(first, BATCH)
+            cols = batch_cols(i, c)[:, g0 * K_PASS : (g0 + count) * K_PASS]
+            z = ring.tile([P, count, PACK, P], F32, name="z")
             nc.vector.tensor_scalar(
-                out=z[:], in0=batch_cols(i, c).rearrange("k (g p t) -> k g t p", p=P, t=PACK),
+                out=z[:], in0=cols.rearrange("k (g p t) -> k g t p", p=P, t=PACK),
                 scalar1=mean, scalar2=rstd, op0=ALU.subtract, op1=ALU.mult,
             )
             live["z", s] = z
 
         def transpose(s):
             banks = []
-            for g in range(BATCH):
+            for g in range(order[s][2]):
                 z_turned = turned.tile([P, PACK, P], F32, tag="turned")
                 for t in range(PACK):
                     nc.tensor.transpose(z_turned[:, t, :], live["z", s][:, g, t, :], ident[:])
@@ -206,11 +257,11 @@ def tile_stulayer_pa_k_kernel(tc, src, ln1_w, ln1_b, w_uvqk_words, w_uvqk_scales
             live["turned", s] = banks
 
         def scale_shift(s):
-            c = order[s][1]
-            y = ring.tile([P, BATCH, PACK, P], BF16, name="y")
-            for g in range(BATCH):
+            first, count = order[s][1:]
+            y = ring.tile([P, count, PACK, P], BF16, name="y")
+            for g in range(count):
                 for t in range(PACK):
-                    at = c * BATCH + g
+                    at = first + g
                     nc.scalar.activation(
                         out=y[:, g, t, :], in_=live["turned", s][g][:, t, :], func=ACT.Identity,
                         scale=gain_col[:, t, at : at + 1], bias=shift_col[:, t, at : at + 1],
@@ -218,7 +269,8 @@ def tile_stulayer_pa_k_kernel(tc, src, ln1_w, ln1_b, w_uvqk_words, w_uvqk_scales
             live["y", s] = y
 
         def regroup(s):
-            grouped = ring.tile([P, BATCH, P, PACK], BF16, name="grouped", align_bytes=64)
+            count = order[s][2]
+            grouped = ring.tile([P, count, P, PACK], BF16, name="grouped", align_bytes=64)
             nc.vector.tensor_copy(
                 out=grouped[:].rearrange("p g (c i) t -> p g c t i", i=4),
                 in_=live["y", s][:].rearrange("p g t (c i) -> p g c t i", i=4),
@@ -226,8 +278,9 @@ def tile_stulayer_pa_k_kernel(tc, src, ln1_w, ln1_b, w_uvqk_words, w_uvqk_scales
             live["grouped", s] = grouped
 
         def quantise(s):
-            words = code_ring.tile([P, BATCH * P], U32, name="x_words", align_bytes=64)
-            scales = code_ring.tile([P, BATCH * P], U8, name="x_scales", align_bytes=64)
+            count = order[s][2]
+            words = code_ring.tile([P, count * P], U32, name="x_words", align_bytes=64)
+            scales = code_ring.tile([P, count * P], U8, name="x_scales", align_bytes=64)
             nc.vector.quantize_mx(
                 out=words[:].bitcast(FP8X4), scales=scales[:],
                 in_=live["grouped", s][:].rearrange("p g k t -> p (g k t)"),
@@ -235,59 +288,74 @@ def tile_stulayer_pa_k_kernel(tc, src, ln1_w, ln1_b, w_uvqk_words, w_uvqk_scales
             live["x", s] = (words, scales)
 
         def multiply(s):
-            i, c = order[s]
+            i, first, count = order[s]
             words, scales = live["x", s]
-            if c == 0:
+            if s == first_of[i]:
                 for h in range(HALVES):
-                    acc[h] = sums.tile([P, N_HALF], F32, name="acc%d" % h)
-            for g in range(BATCH):
-                tokens = slice(g * P, (g + 1) * P)
+                    acc[i, h] = sums.tile([P, N_HALF], F32, name="acc%d_%d" % (i, h))
+            for j in range(count):
+                tokens = slice(j * P, (j + 1) * P)
+                c, g = divmod(first + j, BATCH)
                 for h in range(HALVES):
                     cols = slice(h * N_HALF, (h + 1) * N_HALF)
                     nc.tensor.matmul_mx(
-                        out=acc[h][:],
+                        out=acc[i, h][:],
                         lhsT=words[:, tokens].bitcast(FP8X4),
                         lhsT_scale=scales[:, tokens],
                         rhs=w_words[c][:, g, cols].bitcast(FP8X4),
                         rhs_scale=w_planes[PACK * g : P, c, cols],
-                        start=(c == 0 and g == 0),
-                        stop=(c == BATCHES - 1 and g == BATCH - 1),
+                        start=(s == first_of[i] and j == 0),
+                        stop=(s == last_of[i] and j == count - 1),
                     )
 
         def store(i):
             for h in range(HALVES):
                 cols = slice(h * N_HALF, (h + 1) * N_HALF)
                 result = ring.tile([P, N_HALF], F32, name="result")
-                nc.vector.tensor_tensor(out=result[:], in0=acc[h][:], in1=bias_all[:, cols], op=ALU.add)
+                nc.vector.tensor_tensor(out=result[:], in0=acc[i, h][:], in1=bias_all[:, cols], op=ALU.add)
                 nc.sync.dma_start(out=out_rows[i * P : (i + 1) * P, cols], in_=result[:])
 
-        start_stats(0)
         for c in range(BATCHES):
-            stats_piece(0, c)
+            vector_piece(0, c)
+            for piece in tensor_pieces[0]:
+                if piece[1] == c:
+                    turn_piece(piece)
+                    sum_pieces(GRAM_LAG)
+            if c == BATCHES // 2:
+                make_constants()
+        sum_pieces(0)
         token_stats[0] = finish_stats(0)
-        keep_constants()
         normalise(0)
-        start_stats(1)
-        stats_piece(1, 0)
 
-        steps = len(order)
-        for s in range(steps + MULTIPLY_LAG):
+        ready = first_of[1] - 1
+        pieces = [[] for step in range(ready)]
+        for c in range(BATCHES):
+            pieces[c * ready // BATCHES].append(c)
+        slab_free = max(s for s in range(steps) if order[s][0] == 0 and order[s][1] < SLAB_BATCHES * BATCH)
+
+        for s in range(steps + MULTIPLY_LAG + 1):
+            if s < ready:
+                for c in pieces[s]:
+                    turn_pieces(1, c)
             if s < steps:
                 transpose(s)
+                if s == ready:
+                    token_stats[1] = finish_stats(1)
                 scale_shift(s)
             if 1 <= s <= steps:
                 regroup(s - 1)
-            if s == BATCHES - 1:
-                token_stats[1] = finish_stats(1)
             if s + 1 < steps:
                 normalise(s + 1)
-                if s + 1 == SLAB_BATCHES - 1:
+                if s + 1 == slab_free:
                     w_words.append(load_words(BATCHES - 1))
-            if s + 1 < BATCHES:
-                stats_piece(1, s + 1)
+            if s < ready:
+                for c in pieces[s]:
+                    vector_piece(1, c)
+                sum_pieces(0)
             if 1 <= s <= steps:
                 quantise(s - 1)
-            if s >= MULTIPLY_LAG:
+            if MULTIPLY_LAG <= s < steps + MULTIPLY_LAG:
                 multiply(s - MULTIPLY_LAG)
-                if order[s - MULTIPLY_LAG][1] == BATCHES - 1:
-                    store(order[s - MULTIPLY_LAG][0])
+            for i in range(TOKEN_TILES):
+                if s == last_of[i] + MULTIPLY_LAG + 1:
+                    store(i)

@@ -28,15 +28,27 @@ SLAB_BATCHES = 4
 SLAB_COLS = SLAB_BATCHES * BATCH_COLS
 RESIDENT_SLABS = 11
 PIECE = 512
-PIECE_BLOCKS = PIECE // P
+PIECE_BLOCKS = PIECE // (2 * P)
 VECTOR_PIECES = ((2, 2, 2, 2, 2, 2, 3, 3), (2, 2, 2, 2, 2, 2, 2, 2))
 PIECES = BATCH_COLS // PIECE
 AHEAD = 5
+STORE_SPLIT = 2
+CONST_AT = 1
+HEAD_LAG = 2
+VHEAD = 0
+FIRST_SPLIT = 4
+SRC_CUTS = (8,)
+HEAD_PIECES = 0
+FRONT = 0.25
+TAIL = [(1, 28, 4)]
+VORDER = "nrsq"
 TENSOR_COUNT = [PIECE * sum(PIECES - v for v in row) for row in VECTOR_PIECES]
 STAT_COLS = [6 * sum(row) for row in VECTOR_PIECES]
 GRAM_COLS = P + 2
 RAW_BUFFERS = 4
 GRAM_LAG = 2
+LAG_GROUPS = 6
+CODE_BUFS = 3
 MULTIPLY_LAG = 2
 
 FLOPS = 2 * TOKENS * D * N
@@ -48,7 +60,7 @@ def work_order():
     for c in range(BATCHES - AHEAD):
         items += [(1, BATCH * c, BATCH), (0, BATCH * (AHEAD + c), BATCH)]
     items += [(1, BATCH * c, BATCH) for c in range(BATCHES - AHEAD, BATCHES - 1)]
-    items += [(1, GROUPS - 4, 2), (1, GROUPS - 2, 1), (1, GROUPS - 1, 1)]
+    items += TAIL
     return items
 
 
@@ -65,15 +77,17 @@ def tile_stulayer_pa_k_kernel(tc, src, ln1_w, ln1_b, w_uvqk_words, w_uvqk_scales
         turned = pools.enter_context(tc.psum_pool(name="turned", bufs=4))
         sums = pools.enter_context(tc.psum_pool(name="sums", bufs=1))
 
-        def load_src(i):
-            pair = []
-            for half in range(D // SLAB_COLS):
-                slab = slabs.tile([P, SLAB_COLS], BF16, tag="slab", name="src_slab", align_bytes=64)
-                for b in range(SLAB_BATCHES):
-                    cols = slice(b * BATCH_COLS, (b + 1) * BATCH_COLS)
-                    first = half * SLAB_COLS + b * BATCH_COLS
-                    nc.sync.dma_start(out=slab[:, cols], in_=src_rows[i * P : (i + 1) * P, first : first + BATCH_COLS])
-                pair.append(slab)
+        def load_src(i, batches=range(8), pair=None):
+            if pair is None:
+                pair = [slabs.tile([P, SLAB_COLS], BF16, tag="slab", name="src_slab", align_bytes=64) for half in range(2)]
+            for b in batches:
+                width = BATCH_COLS // (FIRST_SPLIT if i == 0 and b == 0 else 1)
+                for at in range(0, BATCH_COLS, width):
+                    first = b % SLAB_BATCHES * BATCH_COLS + at
+                    nc.sync.dma_start(
+                        out=pair[b // SLAB_BATCHES][:, first : first + width],
+                        in_=src_rows[i * P : (i + 1) * P, b * BATCH_COLS + at : b * BATCH_COLS + at + width],
+                    )
             return pair
 
         def load_scales(c, q):
@@ -94,19 +108,18 @@ def tile_stulayer_pa_k_kernel(tc, src, ln1_w, ln1_b, w_uvqk_words, w_uvqk_scales
             return words
 
         ident = const.tile([P, P], F32)
-        ident_raw = const.tile([P, P], BF16)
         gain_col = const.tile([P, PACK, GROUPS], F32)
         shift_col = const.tile([P, PACK, GROUPS], F32)
         bias_all = const.tile([P, N], BF16)
         w_planes = const.tile([P, BATCHES, N], U8, align_bytes=64)
-        raw_turned = [const.tile([P, PIECE_BLOCKS, GRAM_COLS], BF16, name="raw_turned%d" % n) for n in range(RAW_BUFFERS)]
+        raw_turned = [const.tile([P, PIECE_BLOCKS, GRAM_COLS], F32, name="raw_turned%d" % n) for n in range(RAW_BUFFERS)]
 
         setup = pools.enter_context(tc.tile_pool(name="setup", bufs=1))
         ring = pools.enter_context(tc.tile_pool(name="ring", bufs=2))
-        make_identity(nc, ident_raw[:])
-        for tile in raw_turned:
-            nc.gpsimd.memset(tile[:, :, P:GRAM_COLS], 1.0)
         make_identity(nc, ident[:])
+        for tile in raw_turned:
+            for b in range(PIECE_BLOCKS):
+                nc.gpsimd.memset(tile[:, b, :].bitcast(BF16)[:, 2 * P : 2 * GRAM_COLS], 1.0)
 
         gain_rows = setup.tile([P, K_PASS], BF16)
         nc.gpsimd.memset(gain_rows[64:128, :], 0.0)
@@ -124,12 +137,17 @@ def tile_stulayer_pa_k_kernel(tc, src, ln1_w, ln1_b, w_uvqk_words, w_uvqk_scales
         nc.scalar.activation(out=warm[:], in_=one[:], func=ACT.Sqrt)
 
         nc.gpsimd.memset(w_planes[:].rearrange("p c n -> p (c n)").bitcast(I32), 0)
-        x = [load_src(0), load_src(1)]
+        x = [load_src(0)]
         for q in range(4):
             load_scales(0, q)
-        w_words = [load_words(c) for c in range(BATCHES - 1)]
+        w_words = []
+        x.append(load_src(1, range(0, SRC_CUTS[0])))
+        for c in range(RESIDENT_SLABS - 4):
+            w_words.append(load_words(c))
+            if c + 1 < len(SRC_CUTS):
+                load_src(1, range(SRC_CUTS[c], SRC_CUTS[c + 1]), x[1])
 
-        code_ring = pools.enter_context(tc.tile_pool(name="codes", bufs=MULTIPLY_LAG + 1))
+        code_ring = pools.enter_context(tc.tile_pool(name="codes", bufs=CODE_BUFS))
 
         def make_constants():
             gain_sorted = ring.tile([P, PACK, P], F32, tag="result")
@@ -166,16 +184,17 @@ def tile_stulayer_pa_k_kernel(tc, src, ln1_w, ln1_b, w_uvqk_words, w_uvqk_scales
                 )
 
         tensor_pieces = [[(i, c, j) for c in range(BATCHES) for j in range(VECTOR_PIECES[i][c], PIECES)] for i in range(TOKEN_TILES)]
-        turned_pieces = [0]
 
         raw_ring = []
 
         def turn_piece(piece):
             i, c, j = piece
-            bank = turned.tile([P, PIECE_BLOCKS, P], BF16, tag="turned")
+            words = batch_cols(i, c).bitcast(F32)
+            bank = turned.tile([P, PIECE_BLOCKS, P], F32, tag="turned")
             for b in range(PIECE_BLOCKS):
-                first = j * PIECE + b * P
-                nc.tensor.transpose(bank[:, b, :], batch_cols(i, c)[:, first : first + P], ident_raw[:])
+                first = j * PIECE // 2 + b * P
+                nc.tensor.transpose(bank[:, b, :], words[:, first : first + P], ident[:])
+            assert len(raw_ring) - len(summed) < RAW_BUFFERS
             tile = raw_turned[len(raw_ring) % len(raw_turned)]
             nc.scalar.copy(out=tile[:, :, 0:P], in_=bank[:])
             raw_ring.append((piece, tile))
@@ -188,11 +207,13 @@ def tile_stulayer_pa_k_kernel(tc, src, ln1_w, ln1_b, w_uvqk_words, w_uvqk_scales
             if piece == tensor_pieces[i][0]:
                 gram.append(sums.tile([P, GRAM_COLS], F32, tag="acc%d_0" % i, name="gram"))
             for b in range(PIECE_BLOCKS):
-                nc.tensor.matmul(
-                    gram[i][:], lhsT=tile[:, b, 0:P], rhs=tile[:, b, :],
-                    start=(piece == tensor_pieces[i][0] and b == 0),
-                    stop=(piece == tensor_pieces[i][-1] and b == PIECE_BLOCKS - 1),
-                )
+                for e in range(2):
+                    features = tile[:, b, :].bitcast(BF16)[:, e : 2 * GRAM_COLS : 2]
+                    nc.tensor.matmul(
+                        gram[i][:], lhsT=features[:, 0:P], rhs=features,
+                        start=(piece == tensor_pieces[i][0] and b == 0 and e == 0),
+                        stop=(piece == tensor_pieces[i][-1] and b == PIECE_BLOCKS - 1 and e == 1),
+                    )
             summed.append(piece)
 
         def turn_pieces(i, c):
@@ -293,10 +314,12 @@ def tile_stulayer_pa_k_kernel(tc, src, ln1_w, ln1_b, w_uvqk_words, w_uvqk_scales
             if s == first_of[i]:
                 for h in range(HALVES):
                     acc[i, h] = sums.tile([P, N_HALF], F32, name="acc%d_%d" % (i, h))
-            for j in range(count):
-                tokens = slice(j * P, (j + 1) * P)
-                c, g = divmod(first + j, BATCH)
-                for h in range(HALVES):
+            passes = [(j, h) for j in range(count) for h in range(HALVES)]
+            if s == last_of[i]:
+                passes = sorted(passes, key=lambda jh: jh[1])
+            for j, h in passes:
+                    tokens = slice(j * P, (j + 1) * P)
+                    c, g = divmod(first + j, BATCH)
                     cols = slice(h * N_HALF, (h + 1) * N_HALF)
                     nc.tensor.matmul_mx(
                         out=acc[i, h][:],
@@ -310,52 +333,71 @@ def tile_stulayer_pa_k_kernel(tc, src, ln1_w, ln1_b, w_uvqk_words, w_uvqk_scales
 
         def store(i):
             for h in range(HALVES):
-                cols = slice(h * N_HALF, (h + 1) * N_HALF)
                 result = ring.tile([P, N_HALF], F32, name="result")
-                nc.vector.tensor_tensor(out=result[:], in0=acc[i, h][:], in1=bias_all[:, cols], op=ALU.add)
-                nc.sync.dma_start(out=out_rows[i * P : (i + 1) * P, cols], in_=result[:])
+                width = N_HALF // (STORE_SPLIT if i == 1 and h == 1 else 1)
+                for at in range(0, N_HALF, width):
+                    cols = slice(h * N_HALF + at, h * N_HALF + at + width)
+                    part = slice(at, at + width)
+                    nc.vector.tensor_tensor(out=result[:, part], in0=acc[i, h][:, part], in1=bias_all[:, cols], op=ALU.add)
+                    nc.sync.dma_start(out=out_rows[i * P : (i + 1) * P, cols], in_=result[:, part])
 
         for c in range(BATCHES):
             vector_piece(0, c)
             for piece in tensor_pieces[0]:
                 if piece[1] == c:
                     turn_piece(piece)
-                    sum_pieces(GRAM_LAG)
-            if c == BATCHES // 2:
+                    sum_pieces(HEAD_LAG)
+            if c == CONST_AT:
                 make_constants()
         sum_pieces(0)
+        for c in range(VHEAD):
+            vector_piece(1, c)
         token_stats[0] = finish_stats(0)
+        for piece in tensor_pieces[1][:HEAD_PIECES]:
+            turn_piece(piece)
         normalise(0)
 
         ready = first_of[1] - 1
+        done = [sum(item[2] for item in order[: s + 1]) for s in range(ready)]
         pieces = [[] for step in range(ready)]
         for c in range(BATCHES):
-            pieces[c * ready // BATCHES].append(c)
-        slab_free = max(s for s in range(steps) if order[s][0] == 0 and order[s][1] < SLAB_BATCHES * BATCH)
+            pieces[min(s for s in range(ready) if done[s] * BATCHES >= (c + 1) * done[-1])].append(c)
+        slab_free = [max(s for s in range(steps) if order[s][0] == 0 and order[s][1] < n * SLAB_BATCHES * BATCH) for n in range(1, 13 - RESIDENT_SLABS)]
 
-        for s in range(steps + MULTIPLY_LAG + 1):
+        multiplied = 0
+        stores = []
+        groups_by = [sum(item[2] for item in order[: s + 1]) for s in range(steps)]
+        for s in range(steps + 3):
             if s < ready:
-                for c in pieces[s]:
-                    turn_pieces(1, c)
+                want = round(len(tensor_pieces[1]) * min(1.0, FRONT + (1.0 - FRONT) * done[s] / done[-1]))
+                while len(raw_ring) < len(tensor_pieces[0]) + want and len(raw_ring) - len(summed) < RAW_BUFFERS:
+                    turn_piece(tensor_pieces[1][len(raw_ring) - len(tensor_pieces[0])])
             if s < steps:
                 transpose(s)
                 if s == ready:
                     token_stats[1] = finish_stats(1)
                 scale_shift(s)
-            if 1 <= s <= steps:
-                regroup(s - 1)
-            if s + 1 < steps:
-                normalise(s + 1)
-                if s + 1 == slab_free:
-                    w_words.append(load_words(BATCHES - 1))
             if s < ready:
-                for c in pieces[s]:
-                    vector_piece(1, c)
                 sum_pieces(0)
-            if 1 <= s <= steps:
-                quantise(s - 1)
-            if MULTIPLY_LAG <= s < steps + MULTIPLY_LAG:
-                multiply(s - MULTIPLY_LAG)
-            for i in range(TOKEN_TILES):
-                if s == last_of[i] + MULTIPLY_LAG + 1:
+            for what in VORDER:
+                if what == "r" and 1 <= s <= steps:
+                    regroup(s - 1)
+                if what == "n" and s + 1 < steps:
+                    normalise(s + 1)
+                    if s + 1 in slab_free:
+                        w_words.append(load_words(len(w_words)))
+                if what == "s" and s < ready:
+                    for c in pieces[s]:
+                        if c >= VHEAD:
+                            vector_piece(1, c)
+                if what == "q" and 1 <= s <= steps:
+                    quantise(s - 1)
+            while multiplied < steps and (s >= steps or groups_by[multiplied] + LAG_GROUPS <= groups_by[s]):
+                multiply(multiplied)
+                multiplied += 1
+                for i in range(TOKEN_TILES):
+                    if multiplied == last_of[i] + 1:
+                        stores.append((i, s))
+            for i, at in stores:
+                if s == at + 1:
                     store(i)

@@ -29,14 +29,17 @@ SLAB_COLS = SLAB_BATCHES * BATCH_COLS
 RESIDENT_SLABS = 11
 PIECE = 512
 PIECE_BLOCKS = PIECE // (2 * P)
-VECTOR_PIECES = ((2, 2, 2, 2, 2, 2, 3, 3), (2, 2, 2, 2, 2, 2, 2, 2))
+VECTOR_PIECES = ((2, 2, 2, 2, 2, 2, 2, 3), (2, 2, 2, 2, 2, 2, 2, 1))
 PIECES = BATCH_COLS // PIECE
 AHEAD = 5
+EXTRA = 0
+SRC1_JOIN = 2
+SORT_AT = 0
 STORE_SPLIT = 2
-CONST_AT = 1
+CONST_AT = 2
 HEAD_LAG = 2
 VHEAD = 0
-FIRST_SPLIT = 4
+FIRST_SPLIT = 2
 SRC_CUTS = (8,)
 HEAD_PIECES = 0
 FRONT = 0.25
@@ -57,9 +60,10 @@ FLOPS = 2 * TOKENS * D * N
 def work_order():
     items = [(0, 0, 1), (0, 1, 1), (0, 2, 2)]
     items += [(0, BATCH * c, BATCH) for c in range(1, AHEAD)]
+    items += [(1, BATCH * c, BATCH) for c in range(EXTRA)]
     for c in range(BATCHES - AHEAD):
-        items += [(1, BATCH * c, BATCH), (0, BATCH * (AHEAD + c), BATCH)]
-    items += [(1, BATCH * c, BATCH) for c in range(BATCHES - AHEAD, BATCHES - 1)]
+        items += [(1, BATCH * (EXTRA + c), BATCH), (0, BATCH * (AHEAD + c), BATCH)]
+    items += [(1, BATCH * c, BATCH) for c in range(EXTRA + BATCHES - AHEAD, BATCHES - 1)]
     items += TAIL
     return items
 
@@ -79,9 +83,13 @@ def tile_stulayer_pa_k_kernel(tc, src, ln1_w, ln1_b, w_uvqk_words, w_uvqk_scales
 
         def load_src(i, batches=range(8), pair=None):
             if pair is None:
-                pair = [slabs.tile([P, SLAB_COLS], BF16, tag="slab", name="src_slab", align_bytes=64) for half in range(2)]
+                pair = [slabs.tile([P, SLAB_COLS], BF16, tag="slab", name="src_slab", align_bytes=256) for half in range(2)]
             for b in batches:
-                width = BATCH_COLS // (FIRST_SPLIT if i == 0 and b == 0 else 1)
+                if i == 1 and b % SRC1_JOIN:
+                    continue
+                width = BATCH_COLS // FIRST_SPLIT if i == 0 and b == 0 else BATCH_COLS
+                if i == 1:
+                    width = SRC1_JOIN * BATCH_COLS
                 for at in range(0, BATCH_COLS, width):
                     first = b % SLAB_BATCHES * BATCH_COLS + at
                     nc.sync.dma_start(
@@ -97,7 +105,7 @@ def tile_stulayer_pa_k_kernel(tc, src, ln1_w, ln1_b, w_uvqk_words, w_uvqk_scales
             )
 
         def load_words(c):
-            words = slabs.tile([P, BATCH, N], U32, tag="slab", name="w_slab", align_bytes=64)
+            words = slabs.tile([P, BATCH, N], U32, tag="slab", name="w_slab", align_bytes=256)
             for g in range(BATCH):
                 nc.sync.dma_start(
                     out=words[:, g, :].bitcast(I32),
@@ -111,7 +119,7 @@ def tile_stulayer_pa_k_kernel(tc, src, ln1_w, ln1_b, w_uvqk_words, w_uvqk_scales
         gain_col = const.tile([P, PACK, GROUPS], F32)
         shift_col = const.tile([P, PACK, GROUPS], F32)
         bias_all = const.tile([P, N], BF16)
-        w_planes = const.tile([P, BATCHES, N], U8, align_bytes=64)
+        w_planes = const.tile([P, BATCHES, N], U8, align_bytes=256)
         raw_turned = [const.tile([P, PIECE_BLOCKS, GRAM_COLS], F32, name="raw_turned%d" % n) for n in range(RAW_BUFFERS)]
 
         setup = pools.enter_context(tc.tile_pool(name="setup", bufs=1))
@@ -149,20 +157,25 @@ def tile_stulayer_pa_k_kernel(tc, src, ln1_w, ln1_b, w_uvqk_words, w_uvqk_scales
 
         code_ring = pools.enter_context(tc.tile_pool(name="codes", bufs=CODE_BUFS))
 
-        def make_constants():
-            gain_sorted = ring.tile([P, PACK, P], F32, tag="result")
+        gain_sorted = ring.tile([P, PACK, P], F32, tag="result")
+
+        def sort_gain():
             nc.vector.tensor_copy(out=gain_sorted[:], in_=gain_rows[:].rearrange("r (p t) -> r t p", t=PACK))
+
+        def make_constants():
             gain_turned = sums.tile([P, PACK, P], F32, tag="acc0_1")
             for t in range(PACK):
                 nc.tensor.transpose(gain_turned[:, t, :], gain_sorted[:, t, :], ident[:])
+            spread = []
+            for h in range(HALVES):
+                spread.append(sums.tile([P, N_HALF], F32, tag="acc1_%d" % h, name="spread"))
+                nc.tensor.matmul(
+                    spread[h][:], lhsT=ones[:], rhs=bias_row[:, h * N_HALF : (h + 1) * N_HALF], start=True, stop=True
+                )
             nc.scalar.copy(out=gain_col[:], in_=gain_turned[:, :, 0:GROUPS])
             nc.scalar.copy(out=shift_col[:], in_=gain_turned[:, :, GROUPS : 2 * GROUPS])
             for h in range(HALVES):
-                spread = sums.tile([P, N_HALF], F32, tag="acc1_1")
-                nc.tensor.matmul(
-                    spread[:], lhsT=ones[:], rhs=bias_row[:, h * N_HALF : (h + 1) * N_HALF], start=True, stop=True
-                )
-                nc.scalar.copy(out=bias_all[:, h * N_HALF : (h + 1) * N_HALF], in_=spread[:])
+                nc.scalar.copy(out=bias_all[:, h * N_HALF : (h + 1) * N_HALF], in_=spread[h][:])
 
         def batch_cols(i, c):
             first = (c % SLAB_BATCHES) * BATCH_COLS
@@ -170,6 +183,8 @@ def tile_stulayer_pa_k_kernel(tc, src, ln1_w, ln1_b, w_uvqk_words, w_uvqk_scales
 
         eps = stats.tile([P, 1], F32)
         nc.vector.memset(eps[:], EPS)
+        minus_half = stats.tile([P, 1], F32)
+        nc.vector.memset(minus_half[:], -0.5)
         moments, gram = [], []
         for i in range(TOKEN_TILES):
             moments.append(stats.tile([P, STAT_COLS[i] + 3], F32, name="moments%d" % i))
@@ -242,10 +257,15 @@ def tile_stulayer_pa_k_kernel(tc, src, ln1_w, ln1_b, w_uvqk_words, w_uvqk_scales
             )
             mean_var = stats.tile([P, 2], F32, name="mean_var%d" % i)
             nc.vector.bn_aggr(out=mean_var[:], in_=moments[i][:])
-            std = stats.tile([P, 1], F32, name="std%d" % i)
-            nc.scalar.activation(out=std[:], in_=mean_var[:, 1:2], func=ACT.Sqrt, bias=eps[:])
             rstd = stats.tile([P, 1], F32, name="rstd%d" % i)
-            nc.vector.reciprocal(out=rstd[:], in_=std[:])
+            if i == 0:
+                std = stats.tile([P, 1], F32)
+                nc.scalar.activation(out=std[:], in_=mean_var[:, 1:2], func=ACT.Sqrt, bias=eps[:])
+                nc.vector.reciprocal(out=rstd[:], in_=std[:])
+            else:
+                var_eps = stats.tile([P, 1], F32)
+                nc.vector.tensor_scalar_add(out=var_eps[:], in0=mean_var[:, 1:2], scalar1=EPS)
+                nc.gpsimd.tensor_tensor(out=rstd[:], in0=var_eps[:], in1=minus_half[:], op=ALU.pow)
             return mean_var[:, 0:1], rstd[:]
 
         order = work_order()
@@ -300,8 +320,8 @@ def tile_stulayer_pa_k_kernel(tc, src, ln1_w, ln1_b, w_uvqk_words, w_uvqk_scales
 
         def quantise(s):
             count = order[s][2]
-            words = code_ring.tile([P, count * P], U32, name="x_words", align_bytes=64)
-            scales = code_ring.tile([P, count * P], U8, name="x_scales", align_bytes=64)
+            words = code_ring.tile([P, count * P], U32, name="x_words", align_bytes=256)
+            scales = code_ring.tile([P, count * P], U8, name="x_scales", align_bytes=256)
             nc.vector.quantize_mx(
                 out=words[:].bitcast(FP8X4), scales=scales[:],
                 in_=live["grouped", s][:].rearrange("p g k t -> p (g k t)"),
@@ -347,6 +367,8 @@ def tile_stulayer_pa_k_kernel(tc, src, ln1_w, ln1_b, w_uvqk_words, w_uvqk_scales
                 if piece[1] == c:
                     turn_piece(piece)
                     sum_pieces(HEAD_LAG)
+            if c == SORT_AT:
+                sort_gain()
             if c == CONST_AT:
                 make_constants()
         sum_pieces(0)
@@ -364,21 +386,28 @@ def tile_stulayer_pa_k_kernel(tc, src, ln1_w, ln1_b, w_uvqk_words, w_uvqk_scales
             pieces[min(s for s in range(ready) if done[s] * BATCHES >= (c + 1) * done[-1])].append(c)
         slab_free = [max(s for s in range(steps) if order[s][0] == 0 and order[s][1] < n * SLAB_BATCHES * BATCH) for n in range(1, 13 - RESIDENT_SLABS)]
 
+        def turn_until(want):
+            while len(raw_ring) < len(tensor_pieces[0]) + want and len(raw_ring) - len(summed) < RAW_BUFFERS:
+                turn_piece(tensor_pieces[1][len(raw_ring) - len(tensor_pieces[0])])
+
         multiplied = 0
         stores = []
         groups_by = [sum(item[2] for item in order[: s + 1]) for s in range(steps)]
         for s in range(steps + 3):
             if s < ready:
                 want = round(len(tensor_pieces[1]) * min(1.0, FRONT + (1.0 - FRONT) * done[s] / done[-1]))
-                while len(raw_ring) < len(tensor_pieces[0]) + want and len(raw_ring) - len(summed) < RAW_BUFFERS:
-                    turn_piece(tensor_pieces[1][len(raw_ring) - len(tensor_pieces[0])])
+                turn_until(want)
             if s < steps:
                 transpose(s)
-                if s == ready:
-                    token_stats[1] = finish_stats(1)
                 scale_shift(s)
+                if s == ready:
+                    assert len(summed) == len(tensor_pieces[0]) + len(tensor_pieces[1])
+                    token_stats[1] = finish_stats(1)
             if s < ready:
                 sum_pieces(0)
+                while s == ready - 1 and len(raw_ring) < len(tensor_pieces[0]) + want:
+                    turn_until(want)
+                    sum_pieces(0)
             for what in VORDER:
                 if what == "r" and 1 <= s <= steps:
                     regroup(s - 1)

@@ -32,6 +32,9 @@ PIECE_BLOCKS = PIECE // (2 * P)
 VECTOR_PIECES = ((2, 2, 2, 2, 2, 2, 2, 3), (2, 2, 2, 2, 2, 2, 2, 1))
 PIECES = BATCH_COLS // PIECE
 AHEAD = 5
+YB = 3
+GB = 1
+HEADS = [(0, 0, 2), (0, 2, 2)]
 EXTRA = 0
 SRC1_JOIN = 2
 SORT_AT = 0
@@ -58,7 +61,7 @@ FLOPS = 2 * TOKENS * D * N
 
 
 def work_order():
-    items = [(0, 0, 1), (0, 1, 1), (0, 2, 2)]
+    items = list(HEADS)
     items += [(0, BATCH * c, BATCH) for c in range(1, AHEAD)]
     items += [(1, BATCH * c, BATCH) for c in range(EXTRA)]
     for c in range(BATCHES - AHEAD):
@@ -299,7 +302,7 @@ def tile_stulayer_pa_k_kernel(tc, src, ln1_w, ln1_b, w_uvqk_words, w_uvqk_scales
 
         def scale_shift(s):
             first, count = order[s][1:]
-            y = ring.tile([P, count, PACK, P], BF16, name="y")
+            y = ring.tile([P, count, PACK, P], BF16, name="y", bufs=YB)
             for g in range(count):
                 for t in range(PACK):
                     at = first + g
@@ -311,7 +314,7 @@ def tile_stulayer_pa_k_kernel(tc, src, ln1_w, ln1_b, w_uvqk_words, w_uvqk_scales
 
         def regroup(s):
             count = order[s][2]
-            grouped = ring.tile([P, count, P, PACK], BF16, name="grouped", align_bytes=64)
+            grouped = ring.tile([P, count, P, PACK], BF16, name="grouped", bufs=GB, align_bytes=64)
             nc.vector.tensor_copy(
                 out=grouped[:].rearrange("p g (c i) t -> p g c t i", i=4),
                 in_=live["y", s][:].rearrange("p g t (c i) -> p g c t i", i=4),

@@ -24,15 +24,19 @@ HALVES = N // N_HALF
 BATCH = 4
 BATCH_COLS = BATCH * K_PASS
 BATCHES = GROUPS // BATCH
-SLAB_BATCHES = 4
+SLAB_BATCHES = 2
 SLAB_COLS = SLAB_BATCHES * BATCH_COLS
-RESIDENT_SLABS = 11
+RESIDENT_SLABS = 20
 PIECE = 512
 PIECE_BLOCKS = PIECE // (2 * P)
 VECTOR_PIECES = ((2, 2, 2, 2, 2, 2, 2, 3), (2, 2, 2, 2, 2, 2, 2, 1))
 PIECES = BATCH_COLS // PIECE
 AHEAD = 5
-YB = 3
+NA = 1
+W_GROUPS = 2
+ZB = 3
+HP_LAG = 2
+YB = 4
 GB = 1
 HEADS = [(0, 0, 2), (0, 2, 2)]
 EXTRA = 0
@@ -54,7 +58,7 @@ GRAM_COLS = P + 2
 RAW_BUFFERS = 4
 GRAM_LAG = 2
 LAG_GROUPS = 6
-CODE_BUFS = 3
+CODE_BUFS = 4
 MULTIPLY_LAG = 2
 
 FLOPS = 2 * TOKENS * D * N
@@ -86,7 +90,7 @@ def tile_stulayer_pa_k_kernel(tc, src, ln1_w, ln1_b, w_uvqk_words, w_uvqk_scales
 
         def load_src(i, batches=range(8), pair=None):
             if pair is None:
-                pair = [slabs.tile([P, SLAB_COLS], BF16, tag="slab", name="src_slab", align_bytes=256) for half in range(2)]
+                pair = [slabs.tile([P, SLAB_COLS], BF16, tag="slab", name="src_slab", align_bytes=256) for half in range(BATCHES // SLAB_BATCHES)]
             for b in batches:
                 if i == 1 and b % SRC1_JOIN:
                     continue
@@ -107,15 +111,16 @@ def tile_stulayer_pa_k_kernel(tc, src, ln1_w, ln1_b, w_uvqk_words, w_uvqk_scales
                 in_=w_uvqk_scales[c * BATCH : (c + 1) * BATCH, 4 * q : 4 * q + 4, :].bitcast(I32),
             )
 
-        def load_words(c):
-            words = slabs.tile([P, BATCH, N], U32, tag="slab", name="w_slab", align_bytes=256)
-            for g in range(BATCH):
+        def load_words(u):
+            words = slabs.tile([P, W_GROUPS, N], U32, tag="slab", name="w_slab", align_bytes=256)
+            for g in range(W_GROUPS):
+                at = u * W_GROUPS + g
                 nc.sync.dma_start(
                     out=words[:, g, :].bitcast(I32),
-                    in_=w_uvqk_words[c * BATCH + g].rearrange("p n t -> p (n t)").bitcast(I32),
+                    in_=w_uvqk_words[at].rearrange("p n t -> p (n t)").bitcast(I32),
                 )
-                if c + 1 < BATCHES:
-                    load_scales(c + 1, g)
+                if at // BATCH + 1 < BATCHES:
+                    load_scales(at // BATCH + 1, at % BATCH)
             return words
 
         ident = const.tile([P, P], F32)
@@ -151,12 +156,8 @@ def tile_stulayer_pa_k_kernel(tc, src, ln1_w, ln1_b, w_uvqk_words, w_uvqk_scales
         x = [load_src(0)]
         for q in range(4):
             load_scales(0, q)
-        w_words = []
-        x.append(load_src(1, range(0, SRC_CUTS[0])))
-        for c in range(RESIDENT_SLABS - 4):
-            w_words.append(load_words(c))
-            if c + 1 < len(SRC_CUTS):
-                load_src(1, range(SRC_CUTS[c], SRC_CUTS[c + 1]), x[1])
+        x.append(load_src(1))
+        w_words = [load_words(u) for u in range(RESIDENT_SLABS - 2 * BATCHES // SLAB_BATCHES)]
 
         code_ring = pools.enter_context(tc.tile_pool(name="codes", bufs=CODE_BUFS))
 
@@ -284,7 +285,7 @@ def tile_stulayer_pa_k_kernel(tc, src, ln1_w, ln1_b, w_uvqk_words, w_uvqk_scales
             mean, rstd = token_stats[i]
             c, g0 = divmod(first, BATCH)
             cols = batch_cols(i, c)[:, g0 * K_PASS : (g0 + count) * K_PASS]
-            z = ring.tile([P, count, PACK, P], F32, name="z")
+            z = ring.tile([P, count, PACK, P], F32, name="z", bufs=ZB)
             nc.vector.tensor_scalar(
                 out=z[:], in0=cols.rearrange("k (g p t) -> k g t p", p=P, t=PACK),
                 scalar1=mean, scalar2=rstd, op0=ALU.subtract, op1=ALU.mult,
@@ -348,7 +349,7 @@ def tile_stulayer_pa_k_kernel(tc, src, ln1_w, ln1_b, w_uvqk_words, w_uvqk_scales
                         out=acc[i, h][:],
                         lhsT=words[:, tokens].bitcast(FP8X4),
                         lhsT_scale=scales[:, tokens],
-                        rhs=w_words[c][:, g, cols].bitcast(FP8X4),
+                        rhs=w_words[(first + j) // W_GROUPS][:, (first + j) % W_GROUPS, cols].bitcast(FP8X4),
                         rhs_scale=w_planes[PACK * g : P, c, cols],
                         start=(s == first_of[i] and j == 0),
                         stop=(s == last_of[i] and j == count - 1),
@@ -377,17 +378,20 @@ def tile_stulayer_pa_k_kernel(tc, src, ln1_w, ln1_b, w_uvqk_words, w_uvqk_scales
         sum_pieces(0)
         for c in range(VHEAD):
             vector_piece(1, c)
-        token_stats[0] = finish_stats(0)
         for piece in tensor_pieces[1][:HEAD_PIECES]:
             turn_piece(piece)
-        normalise(0)
+            sum_pieces(HP_LAG)
+        token_stats[0] = finish_stats(0)
+        sum_pieces(0 if HEAD_PIECES else 4)
+        for s in range(NA):
+            normalise(s)
 
-        ready = first_of[1] - 1
+        ready = first_of[1] - NA
         done = [sum(item[2] for item in order[: s + 1]) for s in range(ready)]
         pieces = [[] for step in range(ready)]
         for c in range(BATCHES):
             pieces[min(s for s in range(ready) if done[s] * BATCHES >= (c + 1) * done[-1])].append(c)
-        slab_free = [max(s for s in range(steps) if order[s][0] == 0 and order[s][1] < n * SLAB_BATCHES * BATCH) for n in range(1, 13 - RESIDENT_SLABS)]
+        slab_free = [max(s for s in range(steps) if order[s][0] == 0 and order[s][1] < (n + 1) * SLAB_BATCHES * BATCH) for n in range(GROUPS // W_GROUPS + 2 * BATCHES // SLAB_BATCHES - RESIDENT_SLABS)]
 
         def turn_until(want):
             while len(raw_ring) < len(tensor_pieces[0]) + want and len(raw_ring) - len(summed) < RAW_BUFFERS:
@@ -403,9 +407,6 @@ def tile_stulayer_pa_k_kernel(tc, src, ln1_w, ln1_b, w_uvqk_words, w_uvqk_scales
             if s < steps:
                 transpose(s)
                 scale_shift(s)
-                if s == ready:
-                    assert len(summed) == len(tensor_pieces[0]) + len(tensor_pieces[1])
-                    token_stats[1] = finish_stats(1)
             if s < ready:
                 sum_pieces(0)
                 while s == ready - 1 and len(raw_ring) < len(tensor_pieces[0]) + want:
@@ -414,9 +415,11 @@ def tile_stulayer_pa_k_kernel(tc, src, ln1_w, ln1_b, w_uvqk_words, w_uvqk_scales
             for what in VORDER:
                 if what == "r" and 1 <= s <= steps:
                     regroup(s - 1)
-                if what == "n" and s + 1 < steps:
-                    normalise(s + 1)
-                    if s + 1 in slab_free:
+                if what == "n" and s + NA < steps:
+                    if s + NA == first_of[1]:
+                        token_stats[1] = finish_stats(1)
+                    normalise(s + NA)
+                    for n in range(slab_free.count(s + NA)):
                         w_words.append(load_words(len(w_words)))
                 if what == "s" and s < ready:
                     for c in pieces[s]:

from contextlib import ExitStack

import concourse.mybir as mybir
from concourse.masks import make_identity

F32 = mybir.dt.float32
BF16 = mybir.dt.bfloat16
I32 = mybir.dt.int32
U32 = mybir.dt.uint32
U8 = mybir.dt.uint8
FP8X4 = mybir.dt.float8_e4m3fn_x4
ALU = mybir.AluOpType
ACT = mybir.ActivationFunctionType

P = 128
PACK = 4
K_PASS = P * PACK
TOKENS, D, N = 256, 16384, 1024
EPS = 1e-5
TOKEN_TILES = TOKENS // P
GROUPS = D // K_PASS
N_HALF = 512
HALVES = N // N_HALF
BATCH = 4
BATCH_COLS = BATCH * K_PASS
BATCHES = GROUPS // BATCH
SLAB_BATCHES = 2
SLAB_COLS = SLAB_BATCHES * BATCH_COLS
RESIDENT_SLABS = 20
PIECE = 512
PIECE_BLOCKS = PIECE // (2 * P)
VECTOR_PIECES = ((2, 2, 2, 2, 2, 2, 2, 3), (2, 2, 2, 2, 2, 2, 2, 1))
PIECES = BATCH_COLS // PIECE
AHEAD = 5
NA = 1
W_GROUPS = 2
ZB = 3
HP_LAG = 2
YB = 4
GB = 1
HEADS = [(0, 0, 2), (0, 2, 2)]
EXTRA = 0
SRC1_JOIN = 2
SORT_AT = 0
STORE_SPLIT = 2
CONST_AT = 2
HEAD_LAG = 2
VHEAD = 0
FIRST_SPLIT = 2
SRC_CUTS = (8,)
HEAD_PIECES = 0
FRONT = 0.25
TAIL = [(1, 28, 4)]
VORDER = "nrsq"
TENSOR_COUNT = [PIECE * sum(PIECES - v for v in row) for row in VECTOR_PIECES]
STAT_COLS = [6 * sum(row) for row in VECTOR_PIECES]
GRAM_COLS = P + 2
RAW_BUFFERS = 4
GRAM_LAG = 2
LAG_GROUPS = 6
CODE_BUFS = 4
MULTIPLY_LAG = 2

FLOPS = 2 * TOKENS * D * N


def work_order():
    items = list(HEADS)
    items += [(0, BATCH * c, BATCH) for c in range(1, AHEAD)]
    items += [(1, BATCH * c, BATCH) for c in range(EXTRA)]
    for c in range(BATCHES - AHEAD):
        items += [(1, BATCH * (EXTRA + c), BATCH), (0, BATCH * (AHEAD + c), BATCH)]
    items += [(1, BATCH * c, BATCH) for c in range(EXTRA + BATCHES - AHEAD, BATCHES - 1)]
    items += TAIL
    return items


def tile_stulayer_pa_k_kernel(tc, src, ln1_w, ln1_b, w_uvqk_words, w_uvqk_scales, b_uvqk, out):
    nc = tc.nc
    src_rows = src.rearrange("t b d -> (t b) d")
    out_rows = out.rearrange("t b n -> (t b) n")

    with ExitStack() as pools:
        pools.enter_context(tc.manual_schedule())
        const = pools.enter_context(tc.tile_pool(name="const", bufs=1))
        slabs = pools.enter_context(tc.tile_pool(name="slabs", bufs=RESIDENT_SLABS))
        stats = pools.enter_context(tc.tile_pool(name="stats", bufs=1))
        turned = pools.enter_context(tc.psum_pool(name="turned", bufs=4))
        sums = pools.enter_context(tc.psum_pool(name="sums", bufs=1))

        def load_src(i, batches=range(8), pair=None):
            if pair is None:
                pair = [slabs.tile([P, SLAB_COLS], BF16, tag="slab", name="src_slab", align_bytes=256) for half in range(BATCHES // SLAB_BATCHES)]
            for b in batches:
                if i == 1 and b % SRC1_JOIN:
                    continue
                width = BATCH_COLS // FIRST_SPLIT if i == 0 and b == 0 else BATCH_COLS
                if i == 1:
                    width = SRC1_JOIN * BATCH_COLS
                for at in range(0, BATCH_COLS, width):
                    first = b % SLAB_BATCHES * BATCH_COLS + at
                    nc.sync.dma_start(
                        out=pair[b // SLAB_BATCHES][:, first : first + width],
                        in_=src_rows[i * P : (i + 1) * P, b * BATCH_COLS + at : b * BATCH_COLS + at + width],
                    )
            return pair

        def load_scales(c, q):
            nc.sync.dma_start(
                out=w_planes[32 * q : 32 * q + 16, c, :].bitcast(I32),
                in_=w_uvqk_scales[c * BATCH : (c + 1) * BATCH, 4 * q : 4 * q + 4, :].bitcast(I32),
            )

        def load_words(u):
            words = slabs.tile([P, W_GROUPS, N], U32, tag="slab", name="w_slab", align_bytes=256)
            for g in range(W_GROUPS):
                at = u * W_GROUPS + g
                nc.sync.dma_start(
                    out=words[:, g, :].bitcast(I32),
                    in_=w_uvqk_words[at].rearrange("p n t -> p (n t)").bitcast(I32),
                )
                if at // BATCH + 1 < BATCHES:
                    load_scales(at // BATCH + 1, at % BATCH)
            return words

        ident = const.tile([P, P], F32)
        gain_col = const.tile([P, PACK, GROUPS], F32)
        shift_col = const.tile([P, PACK, GROUPS], F32)
        bias_all = const.tile([P, N], BF16)
        w_planes = const.tile([P, BATCHES, N], U8, align_bytes=256)
        raw_turned = [const.tile([P, PIECE_BLOCKS, GRAM_COLS], F32, name="raw_turned%d" % n) for n in range(RAW_BUFFERS)]

        setup = pools.enter_context(tc.tile_pool(name="setup", bufs=1))
        ring = pools.enter_context(tc.tile_pool(name="ring", bufs=2))
        make_identity(nc, ident[:])
        for tile in raw_turned:
            for b in range(PIECE_BLOCKS):
                nc.gpsimd.memset(tile[:, b, :].bitcast(BF16)[:, 2 * P : 2 * GRAM_COLS], 1.0)

        gain_rows = setup.tile([P, K_PASS], BF16)
        nc.gpsimd.memset(gain_rows[64:128, :], 0.0)
        nc.scalar.dma_start(out=gain_rows[0:GROUPS, :], in_=ln1_w.rearrange("(g k) -> g k", k=K_PASS))
        nc.scalar.dma_start(out=gain_rows[GROUPS : 2 * GROUPS, :], in_=ln1_b.rearrange("(g k) -> g k", k=K_PASS))
        bias_row = ring.tile([P, N], BF16, tag="result")
        nc.vector.memset(bias_row[:], 0.0)
        nc.scalar.dma_start(out=bias_row[0:1, :], in_=b_uvqk.rearrange("(o n) -> o n", o=1))
        ones = setup.tile([P, P], BF16)
        nc.vector.memset(ones[:], 1.0)

        one = setup.tile([P, 1], F32)
        nc.vector.memset(one[:], 1.0)
        warm = setup.tile([P, 1], F32)
        nc.scalar.activation(out=warm[:], in_=one[:], func=ACT.Sqrt)

        nc.gpsimd.memset(w_planes[:].rearrange("p c n -> p (c n)").bitcast(I32), 0)
        x = [load_src(0)]
        for q in range(4):
            load_scales(0, q)
        x.append(load_src(1))
        w_words = [load_words(u) for u in range(RESIDENT_SLABS - 2 * BATCHES // SLAB_BATCHES)]

        code_ring = pools.enter_context(tc.tile_pool(name="codes", bufs=CODE_BUFS))

        gain_sorted = ring.tile([P, PACK, P], F32, tag="result")

        def sort_gain():
            nc.vector.tensor_copy(out=gain_sorted[:], in_=gain_rows[:].rearrange("r (p t) -> r t p", t=PACK))

        def make_constants():
            gain_turned = sums.tile([P, PACK, P], F32, tag="acc0_1")
            for t in range(PACK):
                nc.tensor.transpose(gain_turned[:, t, :], gain_sorted[:, t, :], ident[:])
            spread = []
            for h in range(HALVES):
                spread.append(sums.tile([P, N_HALF], F32, tag="acc1_%d" % h, name="spread"))
                nc.tensor.matmul(
                    spread[h][:], lhsT=ones[:], rhs=bias_row[:, h * N_HALF : (h + 1) * N_HALF], start=True, stop=True
                )
            nc.scalar.copy(out=gain_col[:], in_=gain_turned[:, :, 0:GROUPS])
            nc.scalar.copy(out=shift_col[:], in_=gain_turned[:, :, GROUPS : 2 * GROUPS])
            for h in range(HALVES):
                nc.scalar.copy(out=bias_all[:, h * N_HALF : (h + 1) * N_HALF], in_=spread[h][:])

        def batch_cols(i, c):
            first = (c % SLAB_BATCHES) * BATCH_COLS
            return x[i][c // SLAB_BATCHES][:, first : first + BATCH_COLS]

        eps = stats.tile([P, 1], F32)
        nc.vector.memset(eps[:], EPS)
        minus_half = stats.tile([P, 1], F32)
        nc.vector.memset(minus_half[:], -0.5)
        moments, gram = [], []
        for i in range(TOKEN_TILES):
            moments.append(stats.tile([P, STAT_COLS[i] + 3], F32, name="moments%d" % i))
            nc.vector.memset(moments[i][:, STAT_COLS[i] : STAT_COLS[i] + 1], float(TENSOR_COUNT[i]))
        diagonal = stats.tile([P, P], F32)

        def vector_piece(i, c):
            for j in range(VECTOR_PIECES[i][c]):
                at = 6 * (sum(VECTOR_PIECES[i][:c]) + j)
                nc.vector.bn_stats(
                    out=moments[i][:, at : at + 6], in_=batch_cols(i, c)[:, j * PIECE : (j + 1) * PIECE]
                )

        tensor_pieces = [[(i, c, j) for c in range(BATCHES) for j in range(VECTOR_PIECES[i][c], PIECES)] for i in range(TOKEN_TILES)]

        raw_ring = []

        def turn_piece(piece):
            i, c, j = piece
            words = batch_cols(i, c).bitcast(F32)
            bank = turned.tile([P, PIECE_BLOCKS, P], F32, tag="turned")
            for b in range(PIECE_BLOCKS):
                first = j * PIECE // 2 + b * P
                nc.tensor.transpose(bank[:, b, :], words[:, first : first + P], ident[:])
            assert len(raw_ring) - len(summed) < RAW_BUFFERS
            tile = raw_turned[len(raw_ring) % len(raw_turned)]
            nc.scalar.copy(out=tile[:, :, 0:P], in_=bank[:])
            raw_ring.append((piece, tile))

        summed = []

        def sum_piece():
            piece, tile = raw_ring[len(summed)]
            i = piece[0]
            if piece == tensor_pieces[i][0]:
                gram.append(sums.tile([P, GRAM_COLS], F32, tag="acc%d_0" % i, name="gram"))
            for b in range(PIECE_BLOCKS):
                for e in range(2):
                    features = tile[:, b, :].bitcast(BF16)[:, e : 2 * GRAM_COLS : 2]
                    nc.tensor.matmul(
                        gram[i][:], lhsT=features[:, 0:P], rhs=features,
                        start=(piece == tensor_pieces[i][0] and b == 0 and e == 0),
                        stop=(piece == tensor_pieces[i][-1] and b == PIECE_BLOCKS - 1 and e == 1),
                    )
            summed.append(piece)

        def turn_pieces(i, c):
            for piece in tensor_pieces[i]:
                if piece[1] == c:
                    turn_piece(piece)

        def sum_pieces(lag):
            while len(raw_ring) - len(summed) > lag:
                sum_piece()

        def finish_stats(i):
            mean_of_share = moments[i][:, STAT_COLS[i] + 1 : STAT_COLS[i] + 2]
            total = gram[i][:, P : P + 1]
            negative = stats.tile([P, 1], F32, name="negative%d" % i)
            squares = stats.tile([P, 1], F32, name="squares%d" % i)
            nc.vector.tensor_scalar_mul(out=mean_of_share, in0=total, scalar1=1.0 / TENSOR_COUNT[i])
            nc.vector.tensor_scalar_mul(out=negative[:], in0=total, scalar1=-1.0 / TENSOR_COUNT[i])
            nc.vector.scalar_tensor_tensor(
                out=diagonal[:], in0=gram[i][:, 0:P], scalar=1.0, in1=ident[:], op0=ALU.mult, op1=ALU.mult,
                accum_out=squares[:],
            )
            nc.vector.tensor_scalar(
                out=moments[i][:, STAT_COLS[i] + 2 : STAT_COLS[i] + 3], in0=total,
                scalar1=negative[:], scalar2=squares[:], op0=ALU.mult, op1=ALU.add,
            )
            mean_var = stats.tile([P, 2], F32, name="mean_var%d" % i)
            nc.vector.bn_aggr(out=mean_var[:], in_=moments[i][:])
            rstd = stats.tile([P, 1], F32, name="rstd%d" % i)
            if i == 0:
                std = stats.tile([P, 1], F32)
                nc.scalar.activation(out=std[:], in_=mean_var[:, 1:2], func=ACT.Sqrt, bias=eps[:])
                nc.vector.reciprocal(out=rstd[:], in_=std[:])
            else:
                var_eps = stats.tile([P, 1], F32)
                nc.vector.tensor_scalar_add(out=var_eps[:], in0=mean_var[:, 1:2], scalar1=EPS)
                nc.gpsimd.tensor_tensor(out=rstd[:], in0=var_eps[:], in1=minus_half[:], op=ALU.pow)
            return mean_var[:, 0:1], rstd[:]

        order = work_order()
        steps = len(order)
        first_of = {i: min(s for s in range(steps) if order[s][0] == i) for i in range(TOKEN_TILES)}
        last_of = {i: max(s for s in range(steps) if order[s][0] == i) for i in range(TOKEN_TILES)}
        token_stats = {}
        live = {}
        acc = {}

        def normalise(s):
            i, first, count = order[s]
            mean, rstd = token_stats[i]
            c, g0 = divmod(first, BATCH)
            cols = batch_cols(i, c)[:, g0 * K_PASS : (g0 + count) * K_PASS]
            z = ring.tile([P, count, PACK, P], F32, name="z", bufs=ZB)
            nc.vector.tensor_scalar(
                out=z[:], in0=cols.rearrange("k (g p t) -> k g t p", p=P, t=PACK),
                scalar1=mean, scalar2=rstd, op0=ALU.subtract, op1=ALU.mult,
            )
            live["z", s] = z

        def transpose(s):
            banks = []
            for g in range(order[s][2]):
                z_turned = turned.tile([P, PACK, P], F32, tag="turned")
                for t in range(PACK):
                    nc.tensor.transpose(z_turned[:, t, :], live["z", s][:, g, t, :], ident[:])
                banks.append(z_turned)
            live["turned", s] = banks

        def scale_shift(s):
            first, count = order[s][1:]
            y = ring.tile([P, count, PACK, P], BF16, name="y", bufs=YB)
            for g in range(count):
                for t in range(PACK):
                    at = first + g
                    nc.scalar.activation(
                        out=y[:, g, t, :], in_=live["turned", s][g][:, t, :], func=ACT.Identity,
                        scale=gain_col[:, t, at : at + 1], bias=shift_col[:, t, at : at + 1],
                    )
            live["y", s] = y

        def regroup(s):
            count = order[s][2]
            grouped = ring.tile([P, count, P, PACK], BF16, name="grouped", bufs=GB, align_bytes=64)
            nc.vector.tensor_copy(
                out=grouped[:].rearrange("p g (c i) t -> p g c t i", i=4),
                in_=live["y", s][:].rearrange("p g t (c i) -> p g c t i", i=4),
            )
            live["grouped", s] = grouped

        def quantise(s):
            count = order[s][2]
            words = code_ring.tile([P, count * P], U32, name="x_words", align_bytes=256)
            scales = code_ring.tile([P, count * P], U8, name="x_scales", align_bytes=256)
            nc.vector.quantize_mx(
                out=words[:].bitcast(FP8X4), scales=scales[:],
                in_=live["grouped", s][:].rearrange("p g k t -> p (g k t)"),
            )
            live["x", s] = (words, scales)

        def multiply(s):
            i, first, count = order[s]
            words, scales = live["x", s]
            if s == first_of[i]:
                for h in range(HALVES):
                    acc[i, h] = sums.tile([P, N_HALF], F32, name="acc%d_%d" % (i, h))
            passes = [(j, h) for j in range(count) for h in range(HALVES)]
            if s == last_of[i]:
                passes = sorted(passes, key=lambda jh: jh[1])
            for j, h in passes:
                    tokens = slice(j * P, (j + 1) * P)
                    c, g = divmod(first + j, BATCH)
                    cols = slice(h * N_HALF, (h + 1) * N_HALF)
                    nc.tensor.matmul_mx(
                        out=acc[i, h][:],
                        lhsT=words[:, tokens].bitcast(FP8X4),
                        lhsT_scale=scales[:, tokens],
                        rhs=w_words[(first + j) // W_GROUPS][:, (first + j) % W_GROUPS, cols].bitcast(FP8X4),
                        rhs_scale=w_planes[PACK * g : P, c, cols],
                        start=(s == first_of[i] and j == 0),
                        stop=(s == last_of[i] and j == count - 1),
                    )

        def store(i):
            for h in range(HALVES):
                result = ring.tile([P, N_HALF], F32, name="result")
                width = N_HALF // (STORE_SPLIT if i == 1 and h == 1 else 1)
                for at in range(0, N_HALF, width):
                    cols = slice(h * N_HALF + at, h * N_HALF + at + width)
                    part = slice(at, at + width)
                    nc.vector.tensor_tensor(out=result[:, part], in0=acc[i, h][:, part], in1=bias_all[:, cols], op=ALU.add)
                    nc.sync.dma_start(out=out_rows[i * P : (i + 1) * P, cols], in_=result[:, part])

        for c in range(BATCHES):
            vector_piece(0, c)
            for piece in tensor_pieces[0]:
                if piece[1] == c:
                    turn_piece(piece)
                    sum_pieces(HEAD_LAG)
            if c == SORT_AT:
                sort_gain()
            if c == CONST_AT:
                make_constants()
        sum_pieces(0)
        for c in range(VHEAD):
            vector_piece(1, c)
        for piece in tensor_pieces[1][:HEAD_PIECES]:
            turn_piece(piece)
            sum_pieces(HP_LAG)
        token_stats[0] = finish_stats(0)
        sum_pieces(0 if HEAD_PIECES else 4)
        for s in range(NA):
            normalise(s)

        ready = first_of[1] - NA
        done = [sum(item[2] for item in order[: s + 1]) for s in range(ready)]
        pieces = [[] for step in range(ready)]
        for c in range(BATCHES):
            pieces[min(s for s in range(ready) if done[s] * BATCHES >= (c + 1) * done[-1])].append(c)
        slab_free = [max(s for s in range(steps) if order[s][0] == 0 and order[s][1] < (n + 1) * SLAB_BATCHES * BATCH) for n in range(GROUPS // W_GROUPS + 2 * BATCHES // SLAB_BATCHES - RESIDENT_SLABS)]

        def turn_until(want):
            while len(raw_ring) < len(tensor_pieces[0]) + want and len(raw_ring) - len(summed) < RAW_BUFFERS:
                turn_piece(tensor_pieces[1][len(raw_ring) - len(tensor_pieces[0])])

        multiplied = 0
        stores = []
        groups_by = [sum(item[2] for item in order[: s + 1]) for s in range(steps)]
        for s in range(steps + 3):
            if s < ready:
                want = round(len(tensor_pieces[1]) * min(1.0, FRONT + (1.0 - FRONT) * done[s] / done[-1]))
                turn_until(want)
            if s < steps:
                transpose(s)
                scale_shift(s)
            if s < ready:
                sum_pieces(0)
                while s == ready - 1 and len(raw_ring) < len(tensor_pieces[0]) + want:
                    turn_until(want)
                    sum_pieces(0)
            for what in VORDER:
                if what == "r" and 1 <= s <= steps:
                    regroup(s - 1)
                if what == "n" and s + NA < steps:
                    if s + NA == first_of[1]:
                        token_stats[1] = finish_stats(1)
                    normalise(s + NA)
                    for n in range(slab_free.count(s + NA)):
                        w_words.append(load_words(len(w_words)))
                if what == "s" and s < ready:
                    for c in pieces[s]:
                        if c >= VHEAD:
                            vector_piece(1, c)
                if what == "q" and 1 <= s <= steps:
                    quantise(s - 1)
            while multiplied < steps and (s >= steps or groups_by[multiplied] + LAG_GROUPS <= groups_by[s]):
                multiply(multiplied)
                multiplied += 1
                for i in range(TOKEN_TILES):
                    if multiplied == last_of[i] + 1:
                        stores.append((i, s))
            for i, at in stores:
                if s == at + 1:
                    store(i)
